import numpy as np
import ml_dtypes


def mxq(x, axis, fmt="e4m3"):
    dtype, down = {"e4m3": (ml_dtypes.float8_e4m3fn, 7), "e5m2": (ml_dtypes.float8_e5m2, 14)}[fmt]
    v = np.moveaxis(np.asarray(x, np.float32).astype(ml_dtypes.bfloat16).astype(np.float64), axis, -1)
    blocks = v.reshape(v.shape[:-1] + (-1, 32))
    amax = np.abs(blocks).max(-1, keepdims=True)
    byte = np.maximum(np.where(amax > 0, np.frexp(amax)[1] - 1 + 127, 0) - down, 1)
    scale = np.exp2(byte - 127.0)
    codes = (blocks / scale).astype(np.float32).astype(dtype).astype(np.float64)
    return np.moveaxis((codes * scale).reshape(v.shape), -1, axis)


WIDE = False


def mx_kscale(k):
    if not WIDE:
        return np.ones(k)
    levels = np.array([10, -10, 5, -5, 0])
    a = np.random.permutation(np.resize(levels, k // 512 * 4)).reshape(k // 512, 4)
    idx = np.arange(k)
    return np.exp2(a[idx // 512, idx % 128 // 32])


BF16 = ml_dtypes.bfloat16


def bf(x):
    return np.asarray(x, np.float32).astype(BF16)


def f64(x):
    return np.asarray(x).astype(np.float64)


B, L, E, H = 16, 512, 1024, 256


def skew(m):
    mp = np.pad(m, ((0, 0), (0, 0), (1, 0)))
    return mp.reshape(B, L + 1, L)[:, 1:, :]


def setup_inputs():
    s = mx_kscale(E)
    return {"x": bf(np.random.standard_normal((B, L, E)) * s),
            "q": bf(np.random.standard_normal((B, L, H)) * 1.5),
            "k": bf(np.random.standard_normal((B, L, H))),
            "Wv": bf(np.random.standard_normal((H, E)) / np.sqrt(E) / s[None, :]),
            "rel_emb": bf(np.random.standard_normal((L, H)) / np.sqrt(H))}


def reference(x, q, k, Wv, rel_emb):
    v = mxq(f64(x), 2, "e4m3") @ mxq(f64(Wv), 1, "e4m3").T
    sc = f64(q) @ f64(k).transpose(0, 2, 1) / np.sqrt(H)
    sc = sc + skew(f64(q) @ f64(rel_emb).T)
    causal = np.tril(np.ones((L, L), dtype=bool))
    sc = np.where(causal[None], sc, -np.inf)
    e = np.exp(sc - sc.max(-1, keepdims=True))
    return (mxq(e, 2, "e4m3") @ mxq(v, 1, "e4m3")) / e.sum(-1, keepdims=True)

@@ -1,0 +1,266 @@
+from contextlib import ExitStack
+
+import concourse.mybir as mybir
+from concourse.masks import make_identity
+
+F32 = mybir.dt.float32
+BF16 = mybir.dt.bfloat16
+U32 = mybir.dt.uint32
+U8 = mybir.dt.uint8
+I32 = mybir.dt.int32
+FP8X4 = mybir.dt.float8_e4m3fn_x4
+ALU = mybir.AluOpType
+ACT = mybir.ActivationFunctionType
+
+B, L, E, H = 16, 512, 1024, 256
+P = 128
+NT = L // P
+K_PASS = 4 * P
+X_PASSES = E // K_PASS
+FLOPS = 2 * B * L * (E * H + 3 * L * H)
+
+ROW_W = [P * (i + 1) for i in range(NT)]
+ROW_OFF = [sum(ROW_W[:i]) for i in range(NT)]
+ROW_COLS = sum(ROW_W)
+
+SKEW_PAD = 8
+SKEW_PITCH = ROW_COLS + SKEW_PAD
+SLOT = P * SKEW_PITCH
+N_SLOTS = 4
+LEAD = 3
+
+MASKED = -1.0e30
+
+
+def slot_start(b):
+    return B * L * H - ((B - 1 - b) % N_SLOTS + 1) * SLOT
+
+
+assert all(b - LEAD <= slot_start(b) // (L * H) for b in range(B))
+
+
+def tile_relativeattentionhead_pa_t_kernel(tc, x, q, k, Wv, rel_emb, out):
+    nc = tc.nc
+    out_flat = out.rearrange("b l h -> (b l h)")
+
+    with ExitStack() as ctx:
+        const = ctx.enter_context(tc.tile_pool(name="const", bufs=1))
+        raw_x = ctx.enter_context(tc.tile_pool(name="raw_x", bufs=3))
+        raw_qk = ctx.enter_context(tc.tile_pool(name="raw_qk", bufs=6))
+        heads = ctx.enter_context(tc.tile_pool(name="heads", bufs=LEAD + 3))
+        skewed = ctx.enter_context(tc.tile_pool(name="skewed", bufs=LEAD + 2))
+        work = ctx.enter_context(tc.tile_pool(name="work", bufs=2))
+        small = ctx.enter_context(tc.tile_pool(name="small", bufs=3))
+        ps_score = ctx.enter_context(tc.psum_pool(name="ps_score", bufs=3))
+        ps_tr = ctx.enter_context(tc.psum_pool(name="ps_tr", bufs=3))
+        ps_mx = ctx.enter_context(tc.psum_pool(name="ps_mx", bufs=2))
+
+        ident_f32 = const.tile([P, P], F32)
+        make_identity(nc, ident_f32[:])
+        ident_bf16 = const.tile([P, P], BF16)
+        make_identity(nc, ident_bf16[:])
+
+        rel_rows = [const.tile([P, SKEW_PITCH], F32, name="rel_rows%d" % j) for j in range(N_SLOTS)]
+        for j in range(N_SLOTS):
+            nc.vector.memset(rel_rows[j][:, ROW_COLS:SKEW_PITCH], 0.0)
+
+        e_grouped = [const.tile([P, L * NT], BF16, name="e_grouped%d" % j, align_bytes=64) for j in range(2)]
+        for j in range(2):
+            nc.vector.memset(e_grouped[j][:].bitcast(I32), 0)
+
+        def load_rows(pool, rows, per_partition):
+            raw = pool.tile([P, per_partition * rows.shape[1]], BF16, tag="raw")
+            nc.sync.dma_start(out=raw[:], in_=rows.rearrange("(p t) c -> p (t c)", t=per_partition))
+            return raw
+
+        def head_to_partitions(raw, words):
+            raw_words = raw[:].bitcast(F32)
+            turned = ps_tr.tile([P, NT, P], F32, tag="tr")
+            for t in range(NT):
+                nc.tensor.transpose(turned[:, t, :], raw_words[:, t * P : (t + 1) * P], ident_f32[:])
+            nc.scalar.copy(
+                out=words[:].rearrange("w (p t) -> w p t", t=NT),
+                in_=turned[:].rearrange("w t p -> w p t"),
+            )
+
+        def halves(words):
+            return words[:].bitcast(BF16).rearrange("w (r h) -> w r h", h=2)
+
+        def features_to_partitions(raw, rows_per_partition, grouped):
+            raw_words = raw[:].bitcast(F32)
+            pairs = rows_per_partition // 2
+            dest = grouped[:].bitcast(F32).rearrange(
+                "w (g p a j) -> w g p a j", g=X_PASSES, p=P, a=pairs, j=4
+            )
+            for g in range(X_PASSES):
+                for a in range(pairs):
+                    turned = ps_tr.tile([P, 4, P], F32, tag="tr")
+                    for j in range(4):
+                        t, u = 2 * a + j // 2, j % 2
+                        col = (t * X_PASSES * 2 + g * 2 + u) * P
+                        nc.tensor.transpose(turned[:, j, :], raw_words[:, col : col + P], ident_f32[:])
+                    nc.scalar.copy(out=dest[:, g, :, a, :], in_=turned[:].rearrange("w j p -> w p j"))
+
+        rel_words = const.tile([P, L], F32)
+        head_to_partitions(load_rows(raw_qk, rel_emb, NT), rel_words)
+        rel_t = halves(rel_words)
+
+        w_grouped = const.tile([P, X_PASSES * H * 4], BF16, align_bytes=64)
+        features_to_partitions(load_rows(raw_x, Wv, H // P), H // P, w_grouped)
+        w_codes = const.tile([P, X_PASSES * H], U32, align_bytes=64)
+        w_scales = const.tile([P, X_PASSES * H], U8, align_bytes=64)
+        nc.vector.quantize_mx(out=w_codes[:].bitcast(FP8X4), scales=w_scales[:], in_=w_grouped[:])
+
+        q_raw, k_raw, x_raw = {}, {}, {}
+        q_t, k_t, rel_skewed = {}, {}, {}
+        v_codes, v_scales = {}, {}
+
+        def load_qk(b):
+            q_raw[b] = load_rows(raw_qk, q[b], NT)
+            k_raw[b] = load_rows(raw_qk, k[b], NT)
+
+        def load_x(b):
+            x_raw[b] = load_rows(raw_x, x[b], NT)
+
+        def transpose_qk(b):
+            q_words = heads.tile([P, L], F32)
+            head_to_partitions(q_raw[b], q_words)
+            q_t[b] = halves(q_words)
+            k_words = heads.tile([P, L], F32)
+            head_to_partitions(k_raw[b], k_words)
+            k_t[b] = halves(k_words)
+
+        def q_times(b, i, other, first_col):
+            acc = ps_score.tile([P, L], F32, tag="score")
+            for h in range(2):
+                nc.tensor.matmul(
+                    out=acc[:, 0 : ROW_W[i]],
+                    lhsT=q_t[b][:, i * P : (i + 1) * P, h],
+                    rhs=other[:, first_col : first_col + ROW_W[i], h],
+                    start=(h == 0),
+                    stop=(h == 1),
+                )
+            return acc
+
+        def relative_term(b):
+            rows = rel_rows[(B - 1 - b) % N_SLOTS]
+            for i in range(NT):
+                acc = q_times(b, i, rel_t, L - ROW_W[i])
+                nc.scalar.copy(out=rows[:, ROW_OFF[i] : ROW_OFF[i] + ROW_W[i]], in_=acc[:, 0 : ROW_W[i]])
+            start = slot_start(b)
+            nc.scalar.dma_start(
+                out=out_flat[start : start + SLOT].rearrange("(a u) -> a u", u=SKEW_PITCH), in_=rows[:]
+            )
+            back = skewed.tile([P, ROW_COLS], F32)
+            shifted = out_flat[start + P - 1 : start + P - 1 + P * (SKEW_PITCH - 1)].rearrange(
+                "(a u) -> a u", u=SKEW_PITCH - 1
+            )
+            nc.gpsimd.dma_start(out=back[:], in_=shifted[:, 0:ROW_COLS])
+            for i in range(NT):
+                diag = back[:, ROW_OFF[i] + i * P : ROW_OFF[i] + (i + 1) * P]
+                nc.gpsimd.affine_select(
+                    out=diag, in_=diag, pattern=[[-1, P]], compare_op=ALU.is_ge, fill=MASKED,
+                    base=0, channel_multiplier=1,
+                )
+            rel_skewed[b] = back
+
+        def project_v(b):
+            x_grouped = work.tile([P, L * X_PASSES * 4], BF16, align_bytes=64)
+            features_to_partitions(x_raw[b], NT, x_grouped)
+            x_codes = work.tile([P, X_PASSES * L], U32, align_bytes=64)
+            x_scales = work.tile([P, X_PASSES * L], U8, align_bytes=64)
+            nc.vector.quantize_mx(out=x_codes[:].bitcast(FP8X4), scales=x_scales[:], in_=x_grouped[:])
+
+            v_grouped = work.tile([P, H, NT], BF16, align_bytes=64)
+            for half in range(H // P):
+                acc = ps_mx.tile([P, NT, P], F32, tag="mx")
+                for t in range(NT):
+                    for g in range(X_PASSES):
+                        tok = slice(g * L + t * P, g * L + (t + 1) * P)
+                        col = slice(g * H + half * P, g * H + (half + 1) * P)
+                        nc.tensor.matmul_mx(
+                            out=acc[:, t, :],
+                            lhsT=x_codes[:, tok].bitcast(FP8X4),
+                            lhsT_scale=x_scales[:, tok],
+                            rhs=w_codes[:, col].bitcast(FP8X4),
+                            rhs_scale=w_scales[:, col],
+                            start=(g == 0),
+                            stop=(g == X_PASSES - 1),
+                        )
+                nc.vector.tensor_copy(
+                    out=v_grouped[:, half * P : (half + 1) * P, :], in_=acc[:].rearrange("p t c -> p c t")
+                )
+            codes = work.tile([P, H], U32, align_bytes=64, tag="v_codes")
+            scales = work.tile([P, H], U8, align_bytes=64, tag="v_scales")
+            nc.vector.quantize_mx(
+                out=codes[:].bitcast(FP8X4), scales=scales[:], in_=v_grouped[:].rearrange("p c t -> p (c t)")
+            )
+            v_codes[b], v_scales[b] = codes, scales
+
+        def attend(b):
+            s = rel_skewed[b]
+            neg_max = small.tile([P, NT], F32)
+            row_sum = small.tile([P, NT], F32)
+            e = work.tile([P, ROW_COLS], BF16)
+            for i in range(NT):
+                cols = slice(ROW_OFF[i], ROW_OFF[i] + ROW_W[i])
+                acc = q_times(b, i, k_t[b], 0)
+                nc.vector.scalar_tensor_tensor(
+                    out=s[:, cols], in0=acc[:, 0 : ROW_W[i]], scalar=1.0 / 16.0, in1=s[:, cols],
+                    op0=ALU.mult, op1=ALU.add,
+                )
+                nc.vector.tensor_reduce(
+                    out=neg_max[:, i : i + 1], in_=s[:, cols], axis=mybir.AxisListType.X, op=ALU.max,
+                    negate=True,
+                )
+                nc.scalar.activation(
+                    out=e[:, cols], in_=s[:, cols], func=ACT.Exp, bias=neg_max[:, i : i + 1], scale=1.0,
+                    accum_out=row_sum[:, i : i + 1],
+                )
+            inv_sum = small.tile([P, NT], F32)
+            nc.vector.reciprocal(out=inv_sum[:], in_=row_sum[:])
+
+            grouped = e_grouped[b % 2]
+            by_tile = grouped[:].rearrange("p (i a t) -> p i a t", i=NT, a=P, t=NT)
+            for i in range(NT):
+                turned = ps_tr.tile([P, NT, P], BF16, tag="tr")
+                for t in range(i + 1):
+                    col = ROW_OFF[i] + t * P
+                    nc.tensor.transpose(turned[:, t, :], e[:, col : col + P], ident_bf16[:])
+                nc.vector.tensor_copy(
+                    out=by_tile[:, i, :, 0 : i + 1], in_=turned[:, 0 : i + 1, :].rearrange("p t a -> p a t")
+                )
+            e_codes = work.tile([P, L], U32, align_bytes=64)
+            e_scales = work.tile([P, L], U8, align_bytes=64)
+            nc.vector.quantize_mx(out=e_codes[:].bitcast(FP8X4), scales=e_scales[:], in_=grouped[:])
+
+            result = work.tile([P, NT, H], F32)
+            for pair in range(NT // 2):
+                acc = ps_mx.tile([P, 2, H], F32, tag="mx")
+                for j in range(2):
+                    i = 2 * pair + j
+                    nc.tensor.matmul_mx(
+                        out=acc[:, j, :],
+                        lhsT=e_codes[:, i * P : (i + 1) * P].bitcast(FP8X4),
+                        lhsT_scale=e_scales[:, i * P : (i + 1) * P],
+                        rhs=v_codes[b][:].bitcast(FP8X4),
+                        rhs_scale=v_scales[b][:],
+                        start=True,
+                        stop=True,
+                    )
+                    nc.scalar.activation(
+                        out=result[:, i, :], in_=acc[:, j, :], func=ACT.Copy, scale=inv_sum[:, i : i + 1]
+                    )
+            nc.scalar.dma_start(out=out[b].rearrange("(i a) h -> a i h", a=P), in_=result[:])
+
+        def if_exists(stage, b):
+            if 0 <= b < B:
+                stage(b)
+
+        for n in range(-(LEAD + 2), B):
+            if_exists(load_qk, n + LEAD + 2)
+            if_exists(load_x, n + 2)
+            if_exists(transpose_qk, n + LEAD + 1)
+            if_exists(relative_term, n + LEAD)
+            if_exists(project_v, n + 1)
+            if_exists(attend, n)

@@ -50,10 +50,9 @@ def tile_relativeattentionhead_pa_t_kernel(tc, x, q, k, Wv, rel_emb, out):
         heads = ctx.enter_context(tc.tile_pool(name="heads", bufs=LEAD + 3))
         skewed = ctx.enter_context(tc.tile_pool(name="skewed", bufs=LEAD + 2))
         work = ctx.enter_context(tc.tile_pool(name="work", bufs=2))
+        keep_v = ctx.enter_context(tc.tile_pool(name="keep_v", bufs=3))
         small = ctx.enter_context(tc.tile_pool(name="small", bufs=3))
-        ps_score = ctx.enter_context(tc.psum_pool(name="ps_score", bufs=3))
-        ps_tr = ctx.enter_context(tc.psum_pool(name="ps_tr", bufs=3))
-        ps_mx = ctx.enter_context(tc.psum_pool(name="ps_mx", bufs=2))
+        psum = ctx.enter_context(tc.psum_pool(name="psum", bufs=8))
 
         ident_f32 = const.tile([P, P], F32)
         make_identity(nc, ident_f32[:])
@@ -75,7 +74,7 @@ def tile_relativeattentionhead_pa_t_kernel(tc, x, q, k, Wv, rel_emb, out):
 
         def head_to_partitions(raw, words):
             raw_words = raw[:].bitcast(F32)
-            turned = ps_tr.tile([P, NT, P], F32, tag="tr")
+            turned = psum.tile([P, NT, P], F32, tag="bank")
             for t in range(NT):
                 nc.tensor.transpose(turned[:, t, :], raw_words[:, t * P : (t + 1) * P], ident_f32[:])
             nc.scalar.copy(
@@ -94,7 +93,7 @@ def tile_relativeattentionhead_pa_t_kernel(tc, x, q, k, Wv, rel_emb, out):
             )
             for g in range(X_PASSES):
                 for a in range(pairs):
-                    turned = ps_tr.tile([P, 4, P], F32, tag="tr")
+                    turned = psum.tile([P, 4, P], F32, tag="bank")
                     for j in range(4):
                         t, u = 2 * a + j // 2, j % 2
                         col = (t * X_PASSES * 2 + g * 2 + u) * P
@@ -113,25 +112,18 @@ def tile_relativeattentionhead_pa_t_kernel(tc, x, q, k, Wv, rel_emb, out):
 
         q_raw, k_raw, x_raw = {}, {}, {}
         q_t, k_t, rel_skewed = {}, {}, {}
-        v_codes, v_scales = {}, {}
+        x_grouped, v_codes, v_scales = {}, {}, {}
+        e_rows, row_sum, e_codes, e_scales = {}, {}, {}, {}
 
-        def load_qk(b):
-            q_raw[b] = load_rows(raw_qk, q[b], NT)
-            k_raw[b] = load_rows(raw_qk, k[b], NT)
-
-        def load_x(b):
-            x_raw[b] = load_rows(raw_x, x[b], NT)
-
-        def transpose_qk(b):
-            q_words = heads.tile([P, L], F32)
-            head_to_partitions(q_raw[b], q_words)
-            q_t[b] = halves(q_words)
-            k_words = heads.tile([P, L], F32)
-            head_to_partitions(k_raw[b], k_words)
-            k_t[b] = halves(k_words)
+        def load(b_qk, b_x):
+            if 0 <= b_qk < B:
+                q_raw[b_qk] = load_rows(raw_qk, q[b_qk], NT)
+                k_raw[b_qk] = load_rows(raw_qk, k[b_qk], NT)
+            if 0 <= b_x < B:
+                x_raw[b_x] = load_rows(raw_x, x[b_x], NT)
 
         def q_times(b, i, other, first_col):
-            acc = ps_score.tile([P, L], F32, tag="score")
+            acc = psum.tile([P, L], F32, tag="bank")
             for h in range(2):
                 nc.tensor.matmul(
                     out=acc[:, 0 : ROW_W[i]],
@@ -142,14 +134,30 @@ def tile_relativeattentionhead_pa_t_kernel(tc, x, q, k, Wv, rel_emb, out):
                 )
             return acc
 
-        def relative_term(b):
+        def softmax_numerators(b, i, acc, neg_max):
+            cols = slice(ROW_OFF[i], ROW_OFF[i] + ROW_W[i])
+            s = rel_skewed[b]
+            nc.vector.scalar_tensor_tensor(
+                out=s[:, cols], in0=acc[:, 0 : ROW_W[i]], scalar=1.0 / 16.0, in1=s[:, cols],
+                op0=ALU.mult, op1=ALU.add,
+            )
+            nc.vector.tensor_reduce(
+                out=neg_max[:, i : i + 1], in_=s[:, cols], axis=mybir.AxisListType.X, op=ALU.max, negate=True
+            )
+            nc.scalar.activation(
+                out=e_rows[b][:, cols], in_=s[:, cols], func=ACT.Exp, bias=neg_max[:, i : i + 1], scale=1.0,
+                accum_out=row_sum[b][:, i : i + 1],
+            )
+
+        def park_relative_rows(b, i, acc):
             rows = rel_rows[(B - 1 - b) % N_SLOTS]
-            for i in range(NT):
-                acc = q_times(b, i, rel_t, L - ROW_W[i])
-                nc.scalar.copy(out=rows[:, ROW_OFF[i] : ROW_OFF[i] + ROW_W[i]], in_=acc[:, 0 : ROW_W[i]])
+            nc.scalar.copy(out=rows[:, ROW_OFF[i] : ROW_OFF[i] + ROW_W[i]], in_=acc[:, 0 : ROW_W[i]])
+
+        def skew(b):
             start = slot_start(b)
-            nc.scalar.dma_start(
-                out=out_flat[start : start + SLOT].rearrange("(a u) -> a u", u=SKEW_PITCH), in_=rows[:]
+            nc.sync.dma_start(
+                out=out_flat[start : start + SLOT].rearrange("(a u) -> a u", u=SKEW_PITCH),
+                in_=rel_rows[(B - 1 - b) % N_SLOTS][:],
             )
             back = skewed.tile([P, ROW_COLS], F32)
             shifted = out_flat[start + P - 1 : start + P - 1 + P * (SKEW_PITCH - 1)].rearrange(
@@ -164,16 +172,80 @@ def tile_relativeattentionhead_pa_t_kernel(tc, x, q, k, Wv, rel_emb, out):
                 )
             rel_skewed[b] = back
 
-        def project_v(b):
-            x_grouped = work.tile([P, L * X_PASSES * 4], BF16, align_bytes=64)
-            features_to_partitions(x_raw[b], NT, x_grouped)
-            x_codes = work.tile([P, X_PASSES * L], U32, align_bytes=64)
-            x_scales = work.tile([P, X_PASSES * L], U8, align_bytes=64)
-            nc.vector.quantize_mx(out=x_codes[:].bitcast(FP8X4), scales=x_scales[:], in_=x_grouped[:])
+        def plain_matmuls(b, b_rel):
+            if 0 <= b < B:
+                neg_max = small.tile([P, NT], F32)
+                row_sum[b] = small.tile([P, NT], F32, name="row_sum")
+                e_rows[b] = work.tile([P, ROW_COLS], BF16, name="e_rows")
+            for i in reversed(range(NT)):
+                if 0 <= b < B:
+                    acc_k = q_times(b, i, k_t[b], 0)
+                if 0 <= b_rel < B:
+                    acc_rel = q_times(b_rel, i, rel_t, L - ROW_W[i])
+                    park_relative_rows(b_rel, i, acc_rel)
+                if 0 <= b < B:
+                    softmax_numerators(b, i, acc_k, neg_max)
+            if 0 <= b_rel < B:
+                skew(b_rel)
 
+        def quantise_x(b):
+            codes = work.tile([P, X_PASSES * L], U32, align_bytes=64, name="x_codes")
+            scales = work.tile([P, X_PASSES * L], U8, align_bytes=64, name="x_scales")
+            nc.vector.quantize_mx(out=codes[:].bitcast(FP8X4), scales=scales[:], in_=x_grouped[b][:])
+            return codes, scales
+
+        def transposes(b_x, b_qk, b):
+            if 0 <= b_x < B:
+                x_grouped[b_x] = work.tile([P, L * X_PASSES * 4], BF16, align_bytes=64, name="x_grouped")
+                features_to_partitions(x_raw[b_x], NT, x_grouped[b_x])
+            if 0 <= b_qk < B:
+                q_words = heads.tile([P, L], F32)
+                head_to_partitions(q_raw[b_qk], q_words)
+                q_t[b_qk] = halves(q_words)
+                k_words = heads.tile([P, L], F32)
+                head_to_partitions(k_raw[b_qk], k_words)
+                k_t[b_qk] = halves(k_words)
+            if 0 <= b < B:
+                grouped = e_grouped[b % 2]
+                by_tile = grouped[:].rearrange("p (i a t) -> p i a t", i=NT, a=P, t=NT)
+                for i in reversed(range(NT)):
+                    turned = psum.tile([P, NT, P], BF16, tag="bank")
+                    for t in range(i + 1):
+                        col = ROW_OFF[i] + t * P
+                        nc.tensor.transpose(turned[:, t, :], e_rows[b][:, col : col + P], ident_bf16[:])
+                    nc.vector.tensor_copy(
+                        out=by_tile[:, i, :, 0 : i + 1], in_=turned[:, 0 : i + 1, :].rearrange("p t a -> p a t")
+                    )
+                e_codes[b] = work.tile([P, L], U32, align_bytes=64, name="e_codes")
+                e_scales[b] = work.tile([P, L], U8, align_bytes=64, name="e_scales")
+                nc.vector.quantize_mx(out=e_codes[b][:].bitcast(FP8X4), scales=e_scales[b][:], in_=grouped[:])
+
+        def weighted_sum(b):
+            inv_sum = small.tile([P, NT], F32)
+            nc.vector.reciprocal(out=inv_sum[:], in_=row_sum[b][:])
+            result = work.tile([P, NT, H], F32)
+            for pair in range(NT // 2):
+                acc = psum.tile([P, 2, H], F32, tag="bank")
+                for j in range(2):
+                    i = 2 * pair + j
+                    nc.tensor.matmul_mx(
+                        out=acc[:, j, :],
+                        lhsT=e_codes[b][:, i * P : (i + 1) * P].bitcast(FP8X4),
+                        lhsT_scale=e_scales[b][:, i * P : (i + 1) * P],
+                        rhs=v_codes[b][:].bitcast(FP8X4),
+                        rhs_scale=v_scales[b][:],
+                        start=True,
+                        stop=True,
+                    )
+                    nc.scalar.activation(
+                        out=result[:, i, :], in_=acc[:, j, :], func=ACT.Copy, scale=inv_sum[:, i : i + 1]
+                    )
+            nc.sync.dma_start(out=out[b].rearrange("(i a) h -> a i h", a=P), in_=result[:])
+
+        def project_v(b, x_codes, x_scales):
             v_grouped = work.tile([P, H, NT], BF16, align_bytes=64)
             for half in range(H // P):
-                acc = ps_mx.tile([P, NT, P], F32, tag="mx")
+                acc = psum.tile([P, NT, P], F32, tag="bank")
                 for t in range(NT):
                     for g in range(X_PASSES):
                         tok = slice(g * L + t * P, g * L + (t + 1) * P)
@@ -190,77 +262,21 @@ def tile_relativeattentionhead_pa_t_kernel(tc, x, q, k, Wv, rel_emb, out):
                 nc.vector.tensor_copy(
                     out=v_grouped[:, half * P : (half + 1) * P, :], in_=acc[:].rearrange("p t c -> p c t")
                 )
-            codes = work.tile([P, H], U32, align_bytes=64, tag="v_codes")
-            scales = work.tile([P, H], U8, align_bytes=64, tag="v_scales")
+            v_codes[b] = keep_v.tile([P, H], U32, align_bytes=64, name="v_codes")
+            v_scales[b] = keep_v.tile([P, H], U8, align_bytes=64, name="v_scales")
             nc.vector.quantize_mx(
-                out=codes[:].bitcast(FP8X4), scales=scales[:], in_=v_grouped[:].rearrange("p c t -> p (c t)")
+                out=v_codes[b][:].bitcast(FP8X4), scales=v_scales[b][:],
+                in_=v_grouped[:].rearrange("p c t -> p (c t)"),
             )
-            v_codes[b], v_scales[b] = codes, scales
 
-        def attend(b):
-            s = rel_skewed[b]
-            neg_max = small.tile([P, NT], F32)
-            row_sum = small.tile([P, NT], F32)
-            e = work.tile([P, ROW_COLS], BF16)
-            for i in range(NT):
-                cols = slice(ROW_OFF[i], ROW_OFF[i] + ROW_W[i])
-                acc = q_times(b, i, k_t[b], 0)
-                nc.vector.scalar_tensor_tensor(
-                    out=s[:, cols], in0=acc[:, 0 : ROW_W[i]], scalar=1.0 / 16.0, in1=s[:, cols],
-                    op0=ALU.mult, op1=ALU.add,
-                )
-                nc.vector.tensor_reduce(
-                    out=neg_max[:, i : i + 1], in_=s[:, cols], axis=mybir.AxisListType.X, op=ALU.max,
-                    negate=True,
-                )
-                nc.scalar.activation(
-                    out=e[:, cols], in_=s[:, cols], func=ACT.Exp, bias=neg_max[:, i : i + 1], scale=1.0,
-                    accum_out=row_sum[:, i : i + 1],
-                )
-            inv_sum = small.tile([P, NT], F32)
-            nc.vector.reciprocal(out=inv_sum[:], in_=row_sum[:])
-
-            grouped = e_grouped[b % 2]
-            by_tile = grouped[:].rearrange("p (i a t) -> p i a t", i=NT, a=P, t=NT)
-            for i in range(NT):
-                turned = ps_tr.tile([P, NT, P], BF16, tag="tr")
-                for t in range(i + 1):
-                    col = ROW_OFF[i] + t * P
-                    nc.tensor.transpose(turned[:, t, :], e[:, col : col + P], ident_bf16[:])
-                nc.vector.tensor_copy(
-                    out=by_tile[:, i, :, 0 : i + 1], in_=turned[:, 0 : i + 1, :].rearrange("p t a -> p a t")
-                )
-            e_codes = work.tile([P, L], U32, align_bytes=64)
-            e_scales = work.tile([P, L], U8, align_bytes=64)
-            nc.vector.quantize_mx(out=e_codes[:].bitcast(FP8X4), scales=e_scales[:], in_=grouped[:])
-
-            result = work.tile([P, NT, H], F32)
-            for pair in range(NT // 2):
-                acc = ps_mx.tile([P, 2, H], F32, tag="mx")
-                for j in range(2):
-                    i = 2 * pair + j
-                    nc.tensor.matmul_mx(
-                        out=acc[:, j, :],
-                        lhsT=e_codes[:, i * P : (i + 1) * P].bitcast(FP8X4),
-                        lhsT_scale=e_scales[:, i * P : (i + 1) * P],
-                        rhs=v_codes[b][:].bitcast(FP8X4),
-                        rhs_scale=v_scales[b][:],
-                        start=True,
-                        stop=True,
-                    )
-                    nc.scalar.activation(
-                        out=result[:, i, :], in_=acc[:, j, :], func=ACT.Copy, scale=inv_sum[:, i : i + 1]
-                    )
-            nc.scalar.dma_start(out=out[b].rearrange("(i a) h -> a i h", a=P), in_=result[:])
-
-        def if_exists(stage, b):
-            if 0 <= b < B:
-                stage(b)
-
-        for n in range(-(LEAD + 2), B):
-            if_exists(load_qk, n + LEAD + 2)
-            if_exists(load_x, n + 2)
-            if_exists(transpose_qk, n + LEAD + 1)
-            if_exists(relative_term, n + LEAD)
-            if_exists(project_v, n + 1)
-            if_exists(attend, n)
+        with tc.manual_schedule():
+            for n in range(-(LEAD + 2), B + 1):
+                load(n + LEAD + 2, n + 3)
+                plain_matmuls(n, n + LEAD)
+                if 0 <= n + 1 < B:
+                    x_codes, x_scales = quantise_x(n + 1)
+                transposes(n + 2, n + LEAD + 1, n)
+                if 0 <= n - 1 < B:
+                    weighted_sum(n - 1)
+                if 0 <= n + 1 < B:
+                    project_v(n + 1, x_codes, x_scales)

@@ -113,7 +113,7 @@ def tile_relativeattentionhead_pa_t_kernel(tc, x, q, k, Wv, rel_emb, out):
         q_raw, k_raw, x_raw = {}, {}, {}
         q_t, k_t, rel_skewed = {}, {}, {}
         x_grouped, v_codes, v_scales = {}, {}, {}
-        e_rows, row_sum, e_codes, e_scales = {}, {}, {}, {}
+        e_rows, row_sum, inv_sum, e_codes, e_scales = {}, {}, {}, {}, {}
 
         def load(b_qk, b_x):
             if 0 <= b_qk < B:
@@ -221,8 +221,6 @@ def tile_relativeattentionhead_pa_t_kernel(tc, x, q, k, Wv, rel_emb, out):
                 nc.vector.quantize_mx(out=e_codes[b][:].bitcast(FP8X4), scales=e_scales[b][:], in_=grouped[:])
 
         def weighted_sum(b):
-            inv_sum = small.tile([P, NT], F32)
-            nc.vector.reciprocal(out=inv_sum[:], in_=row_sum[b][:])
             result = work.tile([P, NT, H], F32)
             for pair in range(NT // 2):
                 acc = psum.tile([P, 2, H], F32, tag="bank")
@@ -237,8 +235,10 @@ def tile_relativeattentionhead_pa_t_kernel(tc, x, q, k, Wv, rel_emb, out):
                         start=True,
                         stop=True,
                     )
+                for j in range(2):
+                    i = 2 * pair + j
                     nc.scalar.activation(
-                        out=result[:, i, :], in_=acc[:, j, :], func=ACT.Copy, scale=inv_sum[:, i : i + 1]
+                        out=result[:, i, :], in_=acc[:, j, :], func=ACT.Copy, scale=inv_sum[b][:, i : i + 1]
                     )
             nc.sync.dma_start(out=out[b].rearrange("(i a) h -> a i h", a=P), in_=result[:])
 
@@ -275,6 +275,9 @@ def tile_relativeattentionhead_pa_t_kernel(tc, x, q, k, Wv, rel_emb, out):
                 plain_matmuls(n, n + LEAD)
                 if 0 <= n + 1 < B:
                     x_codes, x_scales = quantise_x(n + 1)
+                if 0 <= n < B:
+                    inv_sum[n] = small.tile([P, NT], F32, name="inv_sum")
+                    nc.vector.reciprocal(out=inv_sum[n][:], in_=row_sum[n][:])
                 transposes(n + 2, n + LEAD + 1, n)
                 if 0 <= n - 1 < B:
                     weighted_sum(n - 1)

@@ -98,7 +98,7 @@ def tile_relativeattentionhead_pa_t_kernel(tc, x, q, k, Wv, rel_emb, out):
                         t, u = 2 * a + j // 2, j % 2
                         col = (t * X_PASSES * 2 + g * 2 + u) * P
                         nc.tensor.transpose(turned[:, j, :], raw_words[:, col : col + P], ident_f32[:])
-                    nc.scalar.copy(out=dest[:, g, :, a, :], in_=turned[:].rearrange("w j p -> w p j"))
+                    nc.vector.tensor_copy(out=dest[:, g, :, a, :], in_=turned[:].rearrange("w j p -> w p j"))
 
         rel_words = const.tile([P, L], F32)
         head_to_partitions(load_rows(raw_qk, rel_emb, NT), rel_words)
@@ -112,8 +112,8 @@ def tile_relativeattentionhead_pa_t_kernel(tc, x, q, k, Wv, rel_emb, out):
 
         q_raw, k_raw, x_raw = {}, {}, {}
         q_t, k_t, rel_skewed = {}, {}, {}
-        x_grouped, v_codes, v_scales = {}, {}, {}
-        e_rows, row_sum, inv_sum, e_codes, e_scales = {}, {}, {}, {}, {}
+        x_codes, x_scales, v_grouped, v_codes, v_scales = {}, {}, {}, {}, {}
+        e_rows, row_sum, e_codes, e_scales = {}, {}, {}, {}
 
         def load(b_qk, b_x):
             if 0 <= b_qk < B:
@@ -136,16 +136,16 @@ def tile_relativeattentionhead_pa_t_kernel(tc, x, q, k, Wv, rel_emb, out):
 
         def softmax_numerators(b, i, acc, neg_max):
             cols = slice(ROW_OFF[i], ROW_OFF[i] + ROW_W[i])
-            s = rel_skewed[b]
+            neg_s = rel_skewed[b][:, cols]
             nc.vector.scalar_tensor_tensor(
-                out=s[:, cols], in0=acc[:, 0 : ROW_W[i]], scalar=1.0 / 16.0, in1=s[:, cols],
-                op0=ALU.mult, op1=ALU.add,
+                out=neg_s, in0=acc[:, 0 : ROW_W[i]], scalar=-1.0 / 16.0, in1=neg_s, op0=ALU.mult, op1=ALU.subtract
             )
-            nc.vector.tensor_reduce(
-                out=neg_max[:, i : i + 1], in_=s[:, cols], axis=mybir.AxisListType.X, op=ALU.max, negate=True
+            nc.vector.tensor_scalar(
+                out=neg_s, in0=neg_s, scalar1=1.0, scalar2=None, op0=ALU.mult, op1=ALU.min,
+                accum_out=neg_max[:, i : i + 1],
             )
             nc.scalar.activation(
-                out=e_rows[b][:, cols], in_=s[:, cols], func=ACT.Exp, bias=neg_max[:, i : i + 1], scale=1.0,
+                out=e_rows[b][:, cols], in_=neg_s, func=ACT.Exp, bias=neg_max[:, i : i + 1], scale=-1.0,
                 accum_out=row_sum[b][:, i : i + 1],
             )
 
@@ -188,41 +188,62 @@ def tile_relativeattentionhead_pa_t_kernel(tc, x, q, k, Wv, rel_emb, out):
             if 0 <= b_rel < B:
                 skew(b_rel)
 
-        def quantise_x(b):
-            codes = work.tile([P, X_PASSES * L], U32, align_bytes=64, name="x_codes")
-            scales = work.tile([P, X_PASSES * L], U8, align_bytes=64, name="x_scales")
-            nc.vector.quantize_mx(out=codes[:].bitcast(FP8X4), scales=scales[:], in_=x_grouped[b][:])
+        def transpose_x(b):
+            x_grouped = work.tile([P, L * X_PASSES * 4], BF16, align_bytes=64)
+            features_to_partitions(x_raw[b], NT, x_grouped)
+            return x_grouped
+
+        def transpose_qk(b):
+            q_words = heads.tile([P, L], F32)
+            head_to_partitions(q_raw[b], q_words)
+            q_t[b] = halves(q_words)
+            k_words = heads.tile([P, L], F32)
+            head_to_partitions(k_raw[b], k_words)
+            k_t[b] = halves(k_words)
+
+        def transpose_e(b):
+            by_tile = e_grouped[b % 2][:].rearrange("p (i a t) -> p i a t", i=NT, a=P, t=NT)
+            for i in reversed(range(NT)):
+                turned = psum.tile([P, NT, P], BF16, tag="bank")
+                for t in range(i + 1):
+                    col = ROW_OFF[i] + t * P
+                    nc.tensor.transpose(turned[:, t, :], e_rows[b][:, col : col + P], ident_bf16[:])
+                nc.scalar.copy(
+                    out=by_tile[:, i, :, 0 : i + 1], in_=turned[:, 0 : i + 1, :].rearrange("p t a -> p a t")
+                )
+
+        def quantise(pool, grouped, name):
+            n_words = grouped.shape[1] // 4
+            codes = pool.tile([P, n_words], U32, align_bytes=64, name=name + "_codes")
+            scales = pool.tile([P, n_words], U8, align_bytes=64, name=name + "_scales")
+            nc.vector.quantize_mx(out=codes[:].bitcast(FP8X4), scales=scales[:], in_=grouped)
             return codes, scales
 
-        def transposes(b_x, b_qk, b):
-            if 0 <= b_x < B:
-                x_grouped[b_x] = work.tile([P, L * X_PASSES * 4], BF16, align_bytes=64, name="x_grouped")
-                features_to_partitions(x_raw[b_x], NT, x_grouped[b_x])
-            if 0 <= b_qk < B:
-                q_words = heads.tile([P, L], F32)
-                head_to_partitions(q_raw[b_qk], q_words)
-                q_t[b_qk] = halves(q_words)
-                k_words = heads.tile([P, L], F32)
-                head_to_partitions(k_raw[b_qk], k_words)
-                k_t[b_qk] = halves(k_words)
-            if 0 <= b < B:
-                grouped = e_grouped[b % 2]
-                by_tile = grouped[:].rearrange("p (i a t) -> p i a t", i=NT, a=P, t=NT)
-                for i in reversed(range(NT)):
-                    turned = psum.tile([P, NT, P], BF16, tag="bank")
-                    for t in range(i + 1):
-                        col = ROW_OFF[i] + t * P
-                        nc.tensor.transpose(turned[:, t, :], e_rows[b][:, col : col + P], ident_bf16[:])
-                    nc.vector.tensor_copy(
-                        out=by_tile[:, i, :, 0 : i + 1], in_=turned[:, 0 : i + 1, :].rearrange("p t a -> p a t")
-                    )
-                e_codes[b] = work.tile([P, L], U32, align_bytes=64, name="e_codes")
-                e_scales[b] = work.tile([P, L], U8, align_bytes=64, name="e_scales")
-                nc.vector.quantize_mx(out=e_codes[b][:].bitcast(FP8X4), scales=e_scales[b][:], in_=grouped[:])
+        def project_v(b):
+            v_grouped[b] = work.tile([P, H, NT], BF16, align_bytes=64, name="v_grouped")
+            for half in range(H // P):
+                acc = psum.tile([P, NT, P], F32, tag="bank")
+                for t in range(NT):
+                    for g in range(X_PASSES):
+                        tok = slice(g * L + t * P, g * L + (t + 1) * P)
+                        col = slice(g * H + half * P, g * H + (half + 1) * P)
+                        nc.tensor.matmul_mx(
+                            out=acc[:, t, :],
+                            lhsT=x_codes[b][:, tok].bitcast(FP8X4),
+                            lhsT_scale=x_scales[b][:, tok],
+                            rhs=w_codes[:, col].bitcast(FP8X4),
+                            rhs_scale=w_scales[:, col],
+                            start=(g == 0),
+                            stop=(g == X_PASSES - 1),
+                        )
+                nc.scalar.copy(
+                    out=v_grouped[b][:, half * P : (half + 1) * P, :], in_=acc[:].rearrange("p t c -> p c t")
+                )
 
-        def weighted_sum(b):
+        def weighted_sum(b, inv_sum):
             result = work.tile([P, NT, H], F32)
             for pair in range(NT // 2):
+                tiles = slice(2 * pair, 2 * pair + 2)
                 acc = psum.tile([P, 2, H], F32, tag="bank")
                 for j in range(2):
                     i = 2 * pair + j
@@ -235,51 +256,34 @@ def tile_relativeattentionhead_pa_t_kernel(tc, x, q, k, Wv, rel_emb, out):
                         start=True,
                         stop=True,
                     )
-                for j in range(2):
-                    i = 2 * pair + j
-                    nc.scalar.activation(
-                        out=result[:, i, :], in_=acc[:, j, :], func=ACT.Copy, scale=inv_sum[b][:, i : i + 1]
-                    )
-            nc.sync.dma_start(out=out[b].rearrange("(i a) h -> a i h", a=P), in_=result[:])
-
-        def project_v(b, x_codes, x_scales):
-            v_grouped = work.tile([P, H, NT], BF16, align_bytes=64)
-            for half in range(H // P):
-                acc = psum.tile([P, NT, P], F32, tag="bank")
-                for t in range(NT):
-                    for g in range(X_PASSES):
-                        tok = slice(g * L + t * P, g * L + (t + 1) * P)
-                        col = slice(g * H + half * P, g * H + (half + 1) * P)
-                        nc.tensor.matmul_mx(
-                            out=acc[:, t, :],
-                            lhsT=x_codes[:, tok].bitcast(FP8X4),
-                            lhsT_scale=x_scales[:, tok],
-                            rhs=w_codes[:, col].bitcast(FP8X4),
-                            rhs_scale=w_scales[:, col],
-                            start=(g == 0),
-                            stop=(g == X_PASSES - 1),
-                        )
-                nc.vector.tensor_copy(
-                    out=v_grouped[:, half * P : (half + 1) * P, :], in_=acc[:].rearrange("p t c -> p c t")
+                nc.vector.tensor_tensor(
+                    out=result[:, tiles, :], in0=acc[:], in1=inv_sum[:, tiles].unsqueeze(2).to_broadcast([P, 2, H]),
+                    op=ALU.mult,
                 )
-            v_codes[b] = keep_v.tile([P, H], U32, align_bytes=64, name="v_codes")
-            v_scales[b] = keep_v.tile([P, H], U8, align_bytes=64, name="v_scales")
-            nc.vector.quantize_mx(
-                out=v_codes[b][:].bitcast(FP8X4), scales=v_scales[b][:],
-                in_=v_grouped[:].rearrange("p c t -> p (c t)"),
-            )
+            nc.sync.dma_start(out=out[b].rearrange("(i a) h -> a i h", a=P), in_=result[:])
 
         with tc.manual_schedule():
             for n in range(-(LEAD + 2), B + 1):
                 load(n + LEAD + 2, n + 3)
                 plain_matmuls(n, n + LEAD)
-                if 0 <= n + 1 < B:
-                    x_codes, x_scales = quantise_x(n + 1)
+
+                if 0 <= n + 2 < B:
+                    x_grouped = transpose_x(n + 2)
+                if 0 <= n + LEAD + 1 < B:
+                    transpose_qk(n + LEAD + 1)
                 if 0 <= n < B:
-                    inv_sum[n] = small.tile([P, NT], F32, name="inv_sum")
-                    nc.vector.reciprocal(out=inv_sum[n][:], in_=row_sum[n][:])
-                transposes(n + 2, n + LEAD + 1, n)
+                    transpose_e(n)
+
                 if 0 <= n - 1 < B:
-                    weighted_sum(n - 1)
+                    e_codes[n - 1], e_scales[n - 1] = quantise(work, e_grouped[(n - 1) % 2][:], "e")
+                if 0 <= n < B:
+                    v_codes[n], v_scales[n] = quantise(keep_v, v_grouped[n][:].rearrange("p c t -> p (c t)"), "v")
+                if 0 <= n + 2 < B:
+                    x_codes[n + 2], x_scales[n + 2] = quantise(work, x_grouped[:], "x")
+
                 if 0 <= n + 1 < B:
-                    project_v(n + 1, x_codes, x_scales)
+                    project_v(n + 1)
+                if 0 <= n - 1 < B:
+                    inv_sum = small.tile([P, NT], F32)
+                    nc.vector.reciprocal(out=inv_sum[:], in_=row_sum[n - 1][:])
+                    weighted_sum(n - 1, inv_sum)

@@ -85,35 +85,34 @@ def tile_relativeattentionhead_pa_t_kernel(tc, x, q, k, Wv, rel_emb, out):
         def halves(words):
             return words[:].bitcast(BF16).rearrange("w (r h) -> w r h", h=2)
 
-        def features_to_partitions(raw, rows_per_partition, grouped):
+        def features_to_partitions(raw, rows_per_partition, grouped, g, a, copy):
             raw_words = raw[:].bitcast(F32)
-            pairs = rows_per_partition // 2
             dest = grouped[:].bitcast(F32).rearrange(
-                "w (g p a j) -> w g p a j", g=X_PASSES, p=P, a=pairs, j=4
+                "w (g p a j) -> w g p a j", g=X_PASSES, p=P, a=rows_per_partition // 2, j=4
             )
-            for g in range(X_PASSES):
-                for a in range(pairs):
-                    turned = psum.tile([P, 4, P], F32, tag="bank")
-                    for j in range(4):
-                        t, u = 2 * a + j // 2, j % 2
-                        col = (t * X_PASSES * 2 + g * 2 + u) * P
-                        nc.tensor.transpose(turned[:, j, :], raw_words[:, col : col + P], ident_f32[:])
-                    nc.vector.tensor_copy(out=dest[:, g, :, a, :], in_=turned[:].rearrange("w j p -> w p j"))
+            turned = psum.tile([P, 4, P], F32, tag="bank")
+            for j in range(4):
+                t, u = 2 * a + j // 2, j % 2
+                col = (t * X_PASSES * 2 + g * 2 + u) * P
+                nc.tensor.transpose(turned[:, j, :], raw_words[:, col : col + P], ident_f32[:])
+            copy(out=dest[:, g, :, a, :], in_=turned[:].rearrange("w j p -> w p j"))
 
         rel_words = const.tile([P, L], F32)
         head_to_partitions(load_rows(raw_qk, rel_emb, NT), rel_words)
         rel_t = halves(rel_words)
 
         w_grouped = const.tile([P, X_PASSES * H * 4], BF16, align_bytes=64)
-        features_to_partitions(load_rows(raw_x, Wv, H // P), H // P, w_grouped)
+        w_raw = load_rows(raw_x, Wv, H // P)
+        for g in range(X_PASSES):
+            features_to_partitions(w_raw, H // P, w_grouped, g, 0, nc.vector.tensor_copy)
         w_codes = const.tile([P, X_PASSES * H], U32, align_bytes=64)
         w_scales = const.tile([P, X_PASSES * H], U8, align_bytes=64)
         nc.vector.quantize_mx(out=w_codes[:].bitcast(FP8X4), scales=w_scales[:], in_=w_grouped[:])
 
         q_raw, k_raw, x_raw = {}, {}, {}
         q_t, k_t, rel_skewed = {}, {}, {}
-        x_codes, x_scales, v_grouped, v_codes, v_scales = {}, {}, {}, {}, {}
-        e_rows, row_sum, e_codes, e_scales = {}, {}, {}, {}
+        x_grouped, x_codes, x_scales, v_grouped, v_codes, v_scales = {}, {}, {}, {}, {}, {}
+        e_rows, neg_max, row_sum, e_codes, e_scales = {}, {}, {}, {}, {}
 
         def load(b_qk, b_x):
             if 0 <= b_qk < B:
@@ -134,18 +133,21 @@ def tile_relativeattentionhead_pa_t_kernel(tc, x, q, k, Wv, rel_emb, out):
                 )
             return acc
 
-        def softmax_numerators(b, i, acc, neg_max):
-            cols = slice(ROW_OFF[i], ROW_OFF[i] + ROW_W[i])
-            neg_s = rel_skewed[b][:, cols]
+        def negated_scores(b, i, acc):
+            neg_s = rel_skewed[b][:, ROW_OFF[i] : ROW_OFF[i] + ROW_W[i]]
             nc.vector.scalar_tensor_tensor(
                 out=neg_s, in0=acc[:, 0 : ROW_W[i]], scalar=-1.0 / 16.0, in1=neg_s, op0=ALU.mult, op1=ALU.subtract
             )
+
+        def softmax_numerators(b, i):
+            cols = slice(ROW_OFF[i], ROW_OFF[i] + ROW_W[i])
+            neg_s = rel_skewed[b][:, cols]
             nc.vector.tensor_scalar(
                 out=neg_s, in0=neg_s, scalar1=1.0, scalar2=None, op0=ALU.mult, op1=ALU.min,
-                accum_out=neg_max[:, i : i + 1],
+                accum_out=neg_max[b][:, i : i + 1],
             )
             nc.scalar.activation(
-                out=e_rows[b][:, cols], in_=neg_s, func=ACT.Exp, bias=neg_max[:, i : i + 1], scale=-1.0,
+                out=e_rows[b][:, cols], in_=neg_s, func=ACT.Exp, bias=neg_max[b][:, i : i + 1], scale=-1.0,
                 accum_out=row_sum[b][:, i : i + 1],
             )
 
@@ -164,7 +166,7 @@ def tile_relativeattentionhead_pa_t_kernel(tc, x, q, k, Wv, rel_emb, out):
                 "(a u) -> a u", u=SKEW_PITCH - 1
             )
             nc.gpsimd.dma_start(out=back[:], in_=shifted[:, 0:ROW_COLS])
-            for i in range(NT):
+            for i in reversed(range(NT)):
                 diag = back[:, ROW_OFF[i] + i * P : ROW_OFF[i] + (i + 1) * P]
                 nc.gpsimd.affine_select(
                     out=diag, in_=diag, pattern=[[-1, P]], compare_op=ALU.is_ge, fill=MASKED,
@@ -172,45 +174,48 @@ def tile_relativeattentionhead_pa_t_kernel(tc, x, q, k, Wv, rel_emb, out):
                 )
             rel_skewed[b] = back
 
-        def plain_matmuls(b, b_rel):
-            if 0 <= b < B:
-                neg_max = small.tile([P, NT], F32)
-                row_sum[b] = small.tile([P, NT], F32, name="row_sum")
-                e_rows[b] = work.tile([P, ROW_COLS], BF16, name="e_rows")
-            for i in reversed(range(NT)):
-                if 0 <= b < B:
-                    acc_k = q_times(b, i, k_t[b], 0)
+        def transpose_e(b, i):
+            by_tile = e_grouped[b % 2][:].rearrange("p (i a t) -> p i a t", i=NT, a=P, t=NT)
+            turned = psum.tile([P, NT, P], BF16, tag="bank")
+            for t in range(i + 1):
+                col = ROW_OFF[i] + t * P
+                nc.tensor.transpose(turned[:, t, :], e_rows[b][:, col : col + P], ident_bf16[:])
+            nc.scalar.copy(out=by_tile[:, i, :, 0 : i + 1], in_=turned[:, 0 : i + 1, :].rearrange("p t a -> p a t"))
+
+        def matmuls_and_transposes(n):
+            b_e, b_rel, b_x, b_qk = n - 1, n + LEAD, n + 2, n + LEAD + 1
+            if 0 <= n < B:
+                neg_max[n] = small.tile([P, NT], F32, name="neg_max")
+                row_sum[n] = small.tile([P, NT], F32, name="row_sum")
+                e_rows[n] = work.tile([P, ROW_COLS], BF16, name="e_rows")
+            if 0 <= b_x < B:
+                x_grouped[b_x] = work.tile([P, L * X_PASSES * 4], BF16, align_bytes=64, name="x_grouped")
+            for r in range(NT):
+                i = NT - 1 - r
+                if 0 <= n < B:
+                    acc_k = q_times(n, i, k_t[n], 0)
+                if 0 <= b_e < B:
+                    transpose_e(b_e, i)
                 if 0 <= b_rel < B:
-                    acc_rel = q_times(b_rel, i, rel_t, L - ROW_W[i])
-                    park_relative_rows(b_rel, i, acc_rel)
-                if 0 <= b < B:
-                    softmax_numerators(b, i, acc_k, neg_max)
+                    park_relative_rows(b_rel, i, q_times(b_rel, i, rel_t, L - ROW_W[i]))
+                if 0 <= n < B:
+                    negated_scores(n, i, acc_k)
+                    if r > 0:
+                        softmax_numerators(n, i + 1)
+                if 0 <= b_x < B:
+                    copy = nc.vector.tensor_copy if r < 2 else nc.scalar.copy
+                    features_to_partitions(x_raw[b_x], NT, x_grouped[b_x], r // 2, r % 2, copy)
+                if 0 <= b_qk < B and r < 2:
+                    words = heads.tile([P, L], F32, tag="q_words" if r == 0 else "k_words")
+                    head_to_partitions(q_raw[b_qk] if r == 0 else k_raw[b_qk], words)
+                    if r == 0:
+                        q_t[b_qk] = halves(words)
+                    else:
+                        k_t[b_qk] = halves(words)
+            if 0 <= n < B:
+                softmax_numerators(n, 0)
             if 0 <= b_rel < B:
                 skew(b_rel)
-
-        def transpose_x(b):
-            x_grouped = work.tile([P, L * X_PASSES * 4], BF16, align_bytes=64)
-            features_to_partitions(x_raw[b], NT, x_grouped)
-            return x_grouped
-
-        def transpose_qk(b):
-            q_words = heads.tile([P, L], F32)
-            head_to_partitions(q_raw[b], q_words)
-            q_t[b] = halves(q_words)
-            k_words = heads.tile([P, L], F32)
-            head_to_partitions(k_raw[b], k_words)
-            k_t[b] = halves(k_words)
-
-        def transpose_e(b):
-            by_tile = e_grouped[b % 2][:].rearrange("p (i a t) -> p i a t", i=NT, a=P, t=NT)
-            for i in reversed(range(NT)):
-                turned = psum.tile([P, NT, P], BF16, tag="bank")
-                for t in range(i + 1):
-                    col = ROW_OFF[i] + t * P
-                    nc.tensor.transpose(turned[:, t, :], e_rows[b][:, col : col + P], ident_bf16[:])
-                nc.scalar.copy(
-                    out=by_tile[:, i, :, 0 : i + 1], in_=turned[:, 0 : i + 1, :].rearrange("p t a -> p a t")
-                )
 
         def quantise(pool, grouped, name):
             n_words = grouped.shape[1] // 4
@@ -236,9 +241,8 @@ def tile_relativeattentionhead_pa_t_kernel(tc, x, q, k, Wv, rel_emb, out):
                             start=(g == 0),
                             stop=(g == X_PASSES - 1),
                         )
-                nc.scalar.copy(
-                    out=v_grouped[b][:, half * P : (half + 1) * P, :], in_=acc[:].rearrange("p t c -> p c t")
-                )
+                copy = nc.scalar.copy if half == 0 else nc.vector.tensor_copy
+                copy(out=v_grouped[b][:, half * P : (half + 1) * P, :], in_=acc[:].rearrange("p t c -> p c t"))
 
         def weighted_sum(b, inv_sum):
             result = work.tile([P, NT, H], F32)
@@ -265,25 +269,18 @@ def tile_relativeattentionhead_pa_t_kernel(tc, x, q, k, Wv, rel_emb, out):
         with tc.manual_schedule():
             for n in range(-(LEAD + 2), B + 1):
                 load(n + LEAD + 2, n + 3)
-                plain_matmuls(n, n + LEAD)
-
-                if 0 <= n + 2 < B:
-                    x_grouped = transpose_x(n + 2)
-                if 0 <= n + LEAD + 1 < B:
-                    transpose_qk(n + LEAD + 1)
-                if 0 <= n < B:
-                    transpose_e(n)
+                matmuls_and_transposes(n)
 
                 if 0 <= n - 1 < B:
+                    inv_sum = small.tile([P, NT], F32)
+                    nc.vector.reciprocal(out=inv_sum[:], in_=row_sum[n - 1][:])
                     e_codes[n - 1], e_scales[n - 1] = quantise(work, e_grouped[(n - 1) % 2][:], "e")
                 if 0 <= n < B:
                     v_codes[n], v_scales[n] = quantise(keep_v, v_grouped[n][:].rearrange("p c t -> p (c t)"), "v")
                 if 0 <= n + 2 < B:
-                    x_codes[n + 2], x_scales[n + 2] = quantise(work, x_grouped[:], "x")
+                    x_codes[n + 2], x_scales[n + 2] = quantise(work, x_grouped[n + 2][:], "x")
 
                 if 0 <= n + 1 < B:
                     project_v(n + 1)
                 if 0 <= n - 1 < B:
-                    inv_sum = small.tile([P, NT], F32)
-                    nc.vector.reciprocal(out=inv_sum[:], in_=row_sum[n - 1][:])
                     weighted_sum(n - 1, inv_sum)

@@ -29,7 +29,7 @@ SLOT = P * SKEW_PITCH
 N_SLOTS = 4
 LEAD = 3
 
-MASKED = -1.0e30
+MASKED = -(2.0**100)
 
 
 def slot_start(b):
@@ -58,6 +58,15 @@ def tile_relativeattentionhead_pa_t_kernel(tc, x, q, k, Wv, rel_emb, out):
         make_identity(nc, ident_f32[:])
         ident_bf16 = const.tile([P, P], BF16)
         make_identity(nc, ident_bf16[:])
+
+        causal_f32 = const.tile([P, P], F32)
+        nc.gpsimd.memset(causal_f32[:], 0.0)
+        nc.gpsimd.affine_select(
+            out=causal_f32[:], in_=causal_f32[:], pattern=[[-1, P]], compare_op=ALU.is_ge, fill=MASKED,
+            base=0, channel_multiplier=1,
+        )
+        causal = const.tile([P, P], BF16)
+        nc.vector.tensor_copy(out=causal[:], in_=causal_f32[:])
 
         rel_rows = [const.tile([P, SKEW_PITCH], F32, name="rel_rows%d" % j) for j in range(N_SLOTS)]
         for j in range(N_SLOTS):
@@ -121,16 +130,25 @@ def tile_relativeattentionhead_pa_t_kernel(tc, x, q, k, Wv, rel_emb, out):
             if 0 <= b_x < B:
                 x_raw[b_x] = load_rows(raw_x, x[b_x], NT)
 
-        def q_times(b, i, other, first_col):
-            acc = psum.tile([P, L], F32, tag="bank")
+        def q_times(acc, b, i, other, cols, masked):
             for h in range(2):
                 nc.tensor.matmul(
-                    out=acc[:, 0 : ROW_W[i]],
-                    lhsT=q_t[b][:, i * P : (i + 1) * P, h],
-                    rhs=other[:, first_col : first_col + ROW_W[i], h],
-                    start=(h == 0),
-                    stop=(h == 1),
+                    out=acc, lhsT=q_t[b][:, i * P : (i + 1) * P, h], rhs=other[:, cols, h],
+                    start=(h == 0), stop=(h == 1 and not masked),
                 )
+            if masked:
+                nc.tensor.matmul(out=acc, lhsT=ident_bf16[:], rhs=causal[:], start=False, stop=True)
+
+        def q_times_k(b, i):
+            acc = psum.tile([P, L], F32, tag="bank")
+            if i > 0:
+                q_times(acc[:, 0 : i * P], b, i, k_t[b], slice(0, i * P), False)
+            q_times(acc[:, i * P : (i + 1) * P], b, i, k_t[b], slice(i * P, (i + 1) * P), True)
+            return acc
+
+        def q_times_rel(b, i):
+            acc = psum.tile([P, L], F32, tag="bank")
+            q_times(acc[:, 0 : ROW_W[i]], b, i, rel_t, slice(L - ROW_W[i], L), False)
             return acc
 
         def negated_scores(b, i, acc):
@@ -139,40 +157,36 @@ def tile_relativeattentionhead_pa_t_kernel(tc, x, q, k, Wv, rel_emb, out):
                 out=neg_s, in0=acc[:, 0 : ROW_W[i]], scalar=-1.0 / 16.0, in1=neg_s, op0=ALU.mult, op1=ALU.subtract
             )
 
-        def softmax_numerators(b, i):
-            cols = slice(ROW_OFF[i], ROW_OFF[i] + ROW_W[i])
-            neg_s = rel_skewed[b][:, cols]
+        def negated_maximum(b, i):
+            neg_s = rel_skewed[b][:, ROW_OFF[i] : ROW_OFF[i] + ROW_W[i]]
             nc.vector.tensor_scalar(
                 out=neg_s, in0=neg_s, scalar1=1.0, scalar2=None, op0=ALU.mult, op1=ALU.min,
                 accum_out=neg_max[b][:, i : i + 1],
             )
+
+        def softmax_numerators(b, i):
+            cols = slice(ROW_OFF[i], ROW_OFF[i] + ROW_W[i])
             nc.scalar.activation(
-                out=e_rows[b][:, cols], in_=neg_s, func=ACT.Exp, bias=neg_max[b][:, i : i + 1], scale=-1.0,
-                accum_out=row_sum[b][:, i : i + 1],
+                out=e_rows[b][:, cols], in_=rel_skewed[b][:, cols], func=ACT.Exp, bias=neg_max[b][:, i : i + 1],
+                scale=-1.0, accum_out=row_sum[b][:, i : i + 1],
             )
 
         def park_relative_rows(b, i, acc):
             rows = rel_rows[(B - 1 - b) % N_SLOTS]
             nc.scalar.copy(out=rows[:, ROW_OFF[i] : ROW_OFF[i] + ROW_W[i]], in_=acc[:, 0 : ROW_W[i]])
 
-        def skew(b):
+        def send_rows(b):
             start = slot_start(b)
             nc.sync.dma_start(
                 out=out_flat[start : start + SLOT].rearrange("(a u) -> a u", u=SKEW_PITCH),
                 in_=rel_rows[(B - 1 - b) % N_SLOTS][:],
             )
-            back = skewed.tile([P, ROW_COLS], F32)
-            shifted = out_flat[start + P - 1 : start + P - 1 + P * (SKEW_PITCH - 1)].rearrange(
-                "(a u) -> a u", u=SKEW_PITCH - 1
-            )
-            nc.gpsimd.dma_start(out=back[:], in_=shifted[:, 0:ROW_COLS])
-            for i in reversed(range(NT)):
-                diag = back[:, ROW_OFF[i] + i * P : ROW_OFF[i] + (i + 1) * P]
-                nc.gpsimd.affine_select(
-                    out=diag, in_=diag, pattern=[[-1, P]], compare_op=ALU.is_ge, fill=MASKED,
-                    base=0, channel_multiplier=1,
-                )
-            rel_skewed[b] = back
+
+        def fetch_skewed(b):
+            start = slot_start(b) + P - 1
+            shifted = out_flat[start : start + P * (SKEW_PITCH - 1)].rearrange("(a u) -> a u", u=SKEW_PITCH - 1)
+            rel_skewed[b] = skewed.tile([P, ROW_COLS], F32, name="rel_skewed")
+            nc.sync.dma_start(out=rel_skewed[b][:], in_=shifted[:, 0:ROW_COLS])
 
         def transpose_e(b, i):
             by_tile = e_grouped[b % 2][:].rearrange("p (i a t) -> p i a t", i=NT, a=P, t=NT)
@@ -193,15 +207,17 @@ def tile_relativeattentionhead_pa_t_kernel(tc, x, q, k, Wv, rel_emb, out):
             for r in range(NT):
                 i = NT - 1 - r
                 if 0 <= n < B:
-                    acc_k = q_times(n, i, k_t[n], 0)
+                    acc_k = q_times_k(n, i)
                 if 0 <= b_e < B:
                     transpose_e(b_e, i)
                 if 0 <= b_rel < B:
-                    park_relative_rows(b_rel, i, q_times(b_rel, i, rel_t, L - ROW_W[i]))
+                    park_relative_rows(b_rel, i, q_times_rel(b_rel, i))
                 if 0 <= n < B:
                     negated_scores(n, i, acc_k)
-                    if r > 0:
-                        softmax_numerators(n, i + 1)
+                    if r >= 1:
+                        negated_maximum(n, i + 1)
+                    if r >= 2:
+                        softmax_numerators(n, i + 2)
                 if 0 <= b_x < B:
                     copy = nc.vector.tensor_copy if r < 2 else nc.scalar.copy
                     features_to_partitions(x_raw[b_x], NT, x_grouped[b_x], r // 2, r % 2, copy)
@@ -213,9 +229,11 @@ def tile_relativeattentionhead_pa_t_kernel(tc, x, q, k, Wv, rel_emb, out):
                     else:
                         k_t[b_qk] = halves(words)
             if 0 <= n < B:
+                negated_maximum(n, 0)
+                softmax_numerators(n, 1)
                 softmax_numerators(n, 0)
             if 0 <= b_rel < B:
-                skew(b_rel)
+                send_rows(b_rel)
 
         def quantise(pool, grouped, name):
             n_words = grouped.shape[1] // 4
@@ -269,6 +287,8 @@ def tile_relativeattentionhead_pa_t_kernel(tc, x, q, k, Wv, rel_emb, out):
         with tc.manual_schedule():
             for n in range(-(LEAD + 2), B + 1):
                 load(n + LEAD + 2, n + 3)
+                if 0 <= n + LEAD - 1 < B:
+                    fetch_skewed(n + LEAD - 1)
                 matmuls_and_transposes(n)
 
                 if 0 <= n - 1 < B:

@@ -45,8 +45,8 @@ def tile_relativeattentionhead_pa_t_kernel(tc, x, q, k, Wv, rel_emb, out):
 
     with ExitStack() as ctx:
         const = ctx.enter_context(tc.tile_pool(name="const", bufs=1))
-        raw_x = ctx.enter_context(tc.tile_pool(name="raw_x", bufs=3))
-        raw_qk = ctx.enter_context(tc.tile_pool(name="raw_qk", bufs=6))
+        raw_x = ctx.enter_context(tc.tile_pool(name="raw_x", bufs=4))
+        raw_qk = ctx.enter_context(tc.tile_pool(name="raw_qk", bufs=8))
         heads = ctx.enter_context(tc.tile_pool(name="heads", bufs=LEAD + 3))
         skewed = ctx.enter_context(tc.tile_pool(name="skewed", bufs=LEAD + 2))
         work = ctx.enter_context(tc.tile_pool(name="work", bufs=2))
@@ -106,18 +106,6 @@ def tile_relativeattentionhead_pa_t_kernel(tc, x, q, k, Wv, rel_emb, out):
                 nc.tensor.transpose(turned[:, j, :], raw_words[:, col : col + P], ident_f32[:])
             copy(out=dest[:, g, :, a, :], in_=turned[:].rearrange("w j p -> w p j"))
 
-        rel_words = const.tile([P, L], F32)
-        head_to_partitions(load_rows(raw_qk, rel_emb, NT), rel_words)
-        rel_t = halves(rel_words)
-
-        w_grouped = const.tile([P, X_PASSES * H * 4], BF16, align_bytes=64)
-        w_raw = load_rows(raw_x, Wv, H // P)
-        for g in range(X_PASSES):
-            features_to_partitions(w_raw, H // P, w_grouped, g, 0, nc.vector.tensor_copy)
-        w_codes = const.tile([P, X_PASSES * H], U32, align_bytes=64)
-        w_scales = const.tile([P, X_PASSES * H], U8, align_bytes=64)
-        nc.vector.quantize_mx(out=w_codes[:].bitcast(FP8X4), scales=w_scales[:], in_=w_grouped[:])
-
         q_raw, k_raw, x_raw = {}, {}, {}
         q_t, k_t, rel_skewed = {}, {}, {}
         x_grouped, x_codes, x_scales, v_grouped, v_codes, v_scales = {}, {}, {}, {}, {}, {}
@@ -129,6 +117,21 @@ def tile_relativeattentionhead_pa_t_kernel(tc, x, q, k, Wv, rel_emb, out):
                 k_raw[b_qk] = load_rows(raw_qk, k[b_qk], NT)
             if 0 <= b_x < B:
                 x_raw[b_x] = load_rows(raw_x, x[b_x], NT)
+
+        rel_raw = load_rows(raw_qk, rel_emb, NT)
+        load(0, -1)
+        w_raw = load_rows(raw_x, Wv, H // P)
+
+        rel_words = const.tile([P, L], F32)
+        head_to_partitions(rel_raw, rel_words)
+        rel_t = halves(rel_words)
+
+        w_grouped = const.tile([P, X_PASSES * H * 4], BF16, align_bytes=64)
+        for g in range(X_PASSES):
+            features_to_partitions(w_raw, H // P, w_grouped, g, 0, nc.vector.tensor_copy)
+        w_codes = const.tile([P, X_PASSES * H], U32, align_bytes=64)
+        w_scales = const.tile([P, X_PASSES * H], U8, align_bytes=64)
+        nc.vector.quantize_mx(out=w_codes[:].bitcast(FP8X4), scales=w_scales[:], in_=w_grouped[:])
 
         def q_times(acc, b, i, other, cols, masked):
             for h in range(2):
@@ -286,10 +289,10 @@ def tile_relativeattentionhead_pa_t_kernel(tc, x, q, k, Wv, rel_emb, out):
 
         with tc.manual_schedule():
             for n in range(-(LEAD + 2), B + 1):
-                load(n + LEAD + 2, n + 3)
                 if 0 <= n + LEAD - 1 < B:
                     fetch_skewed(n + LEAD - 1)
                 matmuls_and_transposes(n)
+                load(n + LEAD + 3, n + 4)
 
                 if 0 <= n - 1 < B:
                     inv_sum = small.tile([P, NT], F32)

@@ -26,17 +26,15 @@ ROW_COLS = sum(ROW_W)
 SKEW_PAD = 8
 SKEW_PITCH = ROW_COLS + SKEW_PAD
 SLOT = P * SKEW_PITCH
-N_SLOTS = 4
+N_SLOTS = 3
 LEAD = 3
+FIRST_STORE_STEP = B - LEAD
 
 MASKED = -(2.0**100)
 
 
 def slot_start(b):
     return B * L * H - ((B - 1 - b) % N_SLOTS + 1) * SLOT
-
-
-assert all(b - LEAD <= slot_start(b) // (L * H) for b in range(B))
 
 
 def tile_relativeattentionhead_pa_t_kernel(tc, x, q, k, Wv, rel_emb, out):
@@ -47,8 +45,9 @@ def tile_relativeattentionhead_pa_t_kernel(tc, x, q, k, Wv, rel_emb, out):
         const = ctx.enter_context(tc.tile_pool(name="const", bufs=1))
         raw_x = ctx.enter_context(tc.tile_pool(name="raw_x", bufs=4))
         raw_qk = ctx.enter_context(tc.tile_pool(name="raw_qk", bufs=8))
-        heads = ctx.enter_context(tc.tile_pool(name="heads", bufs=LEAD + 3))
-        skewed = ctx.enter_context(tc.tile_pool(name="skewed", bufs=LEAD + 2))
+        heads = ctx.enter_context(tc.tile_pool(name="heads", bufs=LEAD + 2))
+        skewed = ctx.enter_context(tc.tile_pool(name="skewed", bufs=LEAD + 1))
+        results = ctx.enter_context(tc.tile_pool(name="results", bufs=FIRST_STORE_STEP + 1))
         work = ctx.enter_context(tc.tile_pool(name="work", bufs=2))
         keep_v = ctx.enter_context(tc.tile_pool(name="keep_v", bufs=3))
         small = ctx.enter_context(tc.tile_pool(name="small", bufs=3))
@@ -109,7 +108,7 @@ def tile_relativeattentionhead_pa_t_kernel(tc, x, q, k, Wv, rel_emb, out):
         q_raw, k_raw, x_raw = {}, {}, {}
         q_t, k_t, rel_skewed = {}, {}, {}
         x_grouped, x_codes, x_scales, v_grouped, v_codes, v_scales = {}, {}, {}, {}, {}, {}
-        e_rows, neg_max, row_sum, e_codes, e_scales = {}, {}, {}, {}, {}
+        e_rows, neg_max, row_sum, e_codes, e_scales, result = {}, {}, {}, {}, {}, {}
 
         def load(b_qk, b_x):
             if 0 <= b_qk < B:
@@ -266,7 +265,7 @@ def tile_relativeattentionhead_pa_t_kernel(tc, x, q, k, Wv, rel_emb, out):
                 copy(out=v_grouped[b][:, half * P : (half + 1) * P, :], in_=acc[:].rearrange("p t c -> p c t"))
 
         def weighted_sum(b, inv_sum):
-            result = work.tile([P, NT, H], F32)
+            result[b] = results.tile([P, NT, H], F32, name="result")
             for pair in range(NT // 2):
                 tiles = slice(2 * pair, 2 * pair + 2)
                 acc = psum.tile([P, 2, H], F32, tag="bank")
@@ -282,10 +281,9 @@ def tile_relativeattentionhead_pa_t_kernel(tc, x, q, k, Wv, rel_emb, out):
                         stop=True,
                     )
                 nc.vector.tensor_tensor(
-                    out=result[:, tiles, :], in0=acc[:], in1=inv_sum[:, tiles].unsqueeze(2).to_broadcast([P, 2, H]),
+                    out=result[b][:, tiles, :], in0=acc[:], in1=inv_sum[:, tiles].unsqueeze(2).to_broadcast([P, 2, H]),
                     op=ALU.mult,
                 )
-            nc.sync.dma_start(out=out[b].rearrange("(i a) h -> a i h", a=P), in_=result[:])
 
         with tc.manual_schedule():
             for n in range(-(LEAD + 2), B + 1):
@@ -307,3 +305,6 @@ def tile_relativeattentionhead_pa_t_kernel(tc, x, q, k, Wv, rel_emb, out):
                     project_v(n + 1)
                 if 0 <= n - 1 < B:
                     weighted_sum(n - 1, inv_sum)
+                if n >= FIRST_STORE_STEP:
+                    for b in range(0 if n == FIRST_STORE_STEP else n - 1, n):
+                        nc.sync.dma_start(out=out[b].rearrange("(i a) h -> a i h", a=P), in_=result[b][:])

@@ -161,10 +161,7 @@ def tile_relativeattentionhead_pa_t_kernel(tc, x, q, k, Wv, rel_emb, out):
 
         def negated_maximum(b, i):
             neg_s = rel_skewed[b][:, ROW_OFF[i] : ROW_OFF[i] + ROW_W[i]]
-            nc.vector.tensor_scalar(
-                out=neg_s, in0=neg_s, scalar1=1.0, scalar2=None, op0=ALU.mult, op1=ALU.min,
-                accum_out=neg_max[b][:, i : i + 1],
-            )
+            nc.vector.tensor_reduce(out=neg_max[b][:, i : i + 1], in_=neg_s, axis=mybir.AxisListType.X, op=ALU.min)
 
         def softmax_numerators(b, i):
             cols = slice(ROW_OFF[i], ROW_OFF[i] + ROW_W[i])

@@ -22,6 +22,9 @@ FLOPS = 2 * B * L * (E * H + 3 * L * H)
 ROW_W = [P * (i + 1) for i in range(NT)]
 ROW_OFF = [sum(ROW_W[:i]) for i in range(NT)]
 ROW_COLS = sum(ROW_W)
+E_W = [2 * P * (i // 2 + 1) for i in range(NT)]
+E_OFF = [sum(E_W[:i]) for i in range(NT)]
+E_COLS = sum(E_W)
 
 SKEW_PAD = 8
 SKEW_PITCH = ROW_COLS + SKEW_PAD
@@ -71,13 +74,24 @@ def tile_relativeattentionhead_pa_t_kernel(tc, x, q, k, Wv, rel_emb, out):
         for j in range(N_SLOTS):
             nc.vector.memset(rel_rows[j][:, ROW_COLS:SKEW_PITCH], 0.0)
 
-        e_grouped = [const.tile([P, L * NT], BF16, name="e_grouped%d" % j, align_bytes=64) for j in range(2)]
+        e_rows = [const.tile([P, E_COLS], BF16, name="e_rows%d" % j) for j in range(2)]
         for j in range(2):
-            nc.vector.memset(e_grouped[j][:].bitcast(I32), 0)
+            nc.vector.memset(e_rows[j][:].bitcast(I32), 0)
+        zeros = const.tile([P, P], F32)
+        nc.vector.memset(zeros[:], 0.0)
 
         def load_rows(pool, rows, per_partition):
             raw = pool.tile([P, per_partition * rows.shape[1]], BF16, tag="raw")
             nc.sync.dma_start(out=raw[:], in_=rows.rearrange("(p t) c -> p (t c)", t=per_partition))
+            return raw
+
+        def load_blocks(pool, rows, blocks, neighbours):
+            n_cols = blocks * neighbours * rows.shape[1]
+            raw = pool.tile([P, n_cols], BF16, tag="raw")
+            nc.sync.dma_start(
+                out=raw[:].rearrange("p (u w) -> p u w", u=blocks),
+                in_=rows.rearrange("(u p h) c -> p u (h c)", u=blocks, h=neighbours),
+            )
             return raw
 
         def head_to_partitions(raw, words):
@@ -93,33 +107,31 @@ def tile_relativeattentionhead_pa_t_kernel(tc, x, q, k, Wv, rel_emb, out):
         def halves(words):
             return words[:].bitcast(BF16).rearrange("w (r h) -> w r h", h=2)
 
-        def features_to_partitions(raw, rows_per_partition, grouped, g, a, copy):
+        def features_to_partitions(raw, slots, grouped, g, a, copy):
             raw_words = raw[:].bitcast(F32)
-            dest = grouped[:].bitcast(F32).rearrange(
-                "w (g p a j) -> w g p a j", g=X_PASSES, p=P, a=rows_per_partition // 2, j=4
-            )
-            turned = psum.tile([P, 4, P], F32, tag="bank")
-            for j in range(4):
-                t, u = 2 * a + j // 2, j % 2
-                col = (t * X_PASSES * 2 + g * 2 + u) * P
-                nc.tensor.transpose(turned[:, j, :], raw_words[:, col : col + P], ident_f32[:])
-            copy(out=dest[:, g, :, a, :], in_=turned[:].rearrange("w j p -> w p j"))
+            dest = grouped[:].bitcast(F32).rearrange("w (g s p u) -> w g s p u", g=X_PASSES, s=slots, u=2)
+            turned = psum.tile([P, 2, 2, P], F32, tag="bank")
+            for j in range(2):
+                for u in range(2):
+                    col = ((2 * a + j) * X_PASSES * 2 + g * 2 + u) * P
+                    nc.tensor.transpose(turned[:, j, u, :], raw_words[:, col : col + P], ident_f32[:])
+            copy(out=dest[:, g, 2 * a : 2 * a + 2, :, :], in_=turned[:].rearrange("w s u p -> w s p u"))
 
         q_raw, k_raw, x_raw = {}, {}, {}
         q_t, k_t, rel_skewed = {}, {}, {}
         x_grouped, x_codes, x_scales, v_grouped, v_codes, v_scales = {}, {}, {}, {}, {}, {}
-        e_rows, neg_max, row_sum, e_codes, e_scales, result = {}, {}, {}, {}, {}, {}
+        neg_max, row_sum, e_grouped, e_codes, e_scales, result = {}, {}, {}, {}, {}, {}
 
         def load(b_qk, b_x):
             if 0 <= b_qk < B:
                 q_raw[b_qk] = load_rows(raw_qk, q[b_qk], NT)
                 k_raw[b_qk] = load_rows(raw_qk, k[b_qk], NT)
             if 0 <= b_x < B:
-                x_raw[b_x] = load_rows(raw_x, x[b_x], NT)
+                x_raw[b_x] = load_blocks(raw_x, x[b_x], 2, 2)
 
         rel_raw = load_rows(raw_qk, rel_emb, NT)
         load(0, -1)
-        w_raw = load_rows(raw_x, Wv, H // P)
+        w_raw = load_blocks(raw_x, Wv, H // P, 1)
 
         rel_words = const.tile([P, L], F32)
         head_to_partitions(rel_raw, rel_words)
@@ -166,7 +178,7 @@ def tile_relativeattentionhead_pa_t_kernel(tc, x, q, k, Wv, rel_emb, out):
         def softmax_numerators(b, i):
             cols = slice(ROW_OFF[i], ROW_OFF[i] + ROW_W[i])
             nc.scalar.activation(
-                out=e_rows[b][:, cols], in_=rel_skewed[b][:, cols], func=ACT.Exp, bias=neg_max[b][:, i : i + 1],
+                out=e_rows[b % 2][:, E_OFF[i] : E_OFF[i] + ROW_W[i]], in_=rel_skewed[b][:, cols], func=ACT.Exp, bias=neg_max[b][:, i : i + 1],
                 scale=-1.0, accum_out=row_sum[b][:, i : i + 1],
             )
 
@@ -187,28 +199,32 @@ def tile_relativeattentionhead_pa_t_kernel(tc, x, q, k, Wv, rel_emb, out):
             rel_skewed[b] = skewed.tile([P, ROW_COLS], F32, name="rel_skewed")
             nc.sync.dma_start(out=rel_skewed[b][:], in_=shifted[:, 0:ROW_COLS])
 
-        def transpose_e(b, i):
-            by_tile = e_grouped[b % 2][:].rearrange("p (i a t) -> p i a t", i=NT, a=P, t=NT)
-            turned = psum.tile([P, NT, P], BF16, tag="bank")
-            for t in range(i + 1):
-                col = ROW_OFF[i] + t * P
-                nc.tensor.transpose(turned[:, t, :], e_rows[b][:, col : col + P], ident_bf16[:])
-            nc.scalar.copy(out=by_tile[:, i, :, 0 : i + 1], in_=turned[:, 0 : i + 1, :].rearrange("p t a -> p a t"))
+        def transpose_e(b, first):
+            words = e_rows[b % 2][:].bitcast(F32)
+            turned = psum.tile([P, 2, 2, P], F32, tag="bank")
+            for j in range(2):
+                for u in range(2):
+                    col = (E_OFF[first + j] + 2 * P * u) // 2
+                    block = words[:, col : col + P] if 2 * P * u < E_W[first + j] else zeros[:]
+                    nc.tensor.transpose(turned[:, j, u, :], block, ident_f32[:])
+            dest = e_grouped[b][:].bitcast(F32).rearrange("p (i a u) -> p i a u", i=NT, u=2)
+            nc.scalar.copy(out=dest[:, first : first + 2, :, :], in_=turned[:].rearrange("p i u a -> p i a u"))
 
         def matmuls_and_transposes(n):
             b_e, b_rel, b_x, b_qk = n - 1, n + LEAD, n + 2, n + LEAD + 1
             if 0 <= n < B:
                 neg_max[n] = small.tile([P, NT], F32, name="neg_max")
                 row_sum[n] = small.tile([P, NT], F32, name="row_sum")
-                e_rows[n] = work.tile([P, ROW_COLS], BF16, name="e_rows")
+            if 0 <= b_e < B:
+                e_grouped[b_e] = work.tile([P, L * NT], BF16, align_bytes=64, name="e_grouped")
             if 0 <= b_x < B:
                 x_grouped[b_x] = work.tile([P, L * X_PASSES * 4], BF16, align_bytes=64, name="x_grouped")
             for r in range(NT):
                 i = NT - 1 - r
                 if 0 <= n < B:
                     acc_k = q_times_k(n, i)
-                if 0 <= b_e < B:
-                    transpose_e(b_e, i)
+                if 0 <= b_e < B and r % 2 == 0:
+                    transpose_e(b_e, 2 - r)
                 if 0 <= b_rel < B:
                     park_relative_rows(b_rel, i, q_times_rel(b_rel, i))
                 if 0 <= n < B:
@@ -292,7 +308,7 @@ def tile_relativeattentionhead_pa_t_kernel(tc, x, q, k, Wv, rel_emb, out):
                 if 0 <= n - 1 < B:
                     inv_sum = small.tile([P, NT], F32)
                     nc.vector.reciprocal(out=inv_sum[:], in_=row_sum[n - 1][:])
-                    e_codes[n - 1], e_scales[n - 1] = quantise(work, e_grouped[(n - 1) % 2][:], "e")
+                    e_codes[n - 1], e_scales[n - 1] = quantise(work, e_grouped[n - 1][:], "e")
                 if 0 <= n < B:
                     v_codes[n], v_scales[n] = quantise(keep_v, v_grouped[n][:].rearrange("p c t -> p (c t)"), "v")
                 if 0 <= n + 2 < B:

@@ -274,8 +274,7 @@ def tile_relativeattentionhead_pa_t_kernel(tc, x, q, k, Wv, rel_emb, out):
                             start=(g == 0),
                             stop=(g == X_PASSES - 1),
                         )
-                copy = nc.scalar.copy if half == 0 else nc.vector.tensor_copy
-                copy(out=v_grouped[b][:, half * P : (half + 1) * P, :], in_=acc[:].rearrange("p t c -> p c t"))
+                nc.scalar.copy(out=v_grouped[b][:, half * P : (half + 1) * P, :], in_=acc[:].rearrange("p t c -> p c t"))
 
         def weighted_sum(b, inv_sum):
             result[b] = results.tile([P, NT, H], F32, name="result")

@@ -29,9 +29,9 @@ E_COLS = sum(E_W)
 SKEW_PAD = 8
 SKEW_PITCH = ROW_COLS + SKEW_PAD
 SLOT = P * SKEW_PITCH
-N_SLOTS = 3
-LEAD = 3
-FIRST_STORE_STEP = B - LEAD
+N_SLOTS = 2
+LEAD = 2
+assert N_SLOTS * SLOT <= LEAD * L * H + L * H
 
 MASKED = -(2.0**100)
 
@@ -50,7 +50,7 @@ def tile_relativeattentionhead_pa_t_kernel(tc, x, q, k, Wv, rel_emb, out):
         raw_qk = ctx.enter_context(tc.tile_pool(name="raw_qk", bufs=8))
         heads = ctx.enter_context(tc.tile_pool(name="heads", bufs=LEAD + 2))
         skewed = ctx.enter_context(tc.tile_pool(name="skewed", bufs=LEAD + 1))
-        results = ctx.enter_context(tc.tile_pool(name="results", bufs=FIRST_STORE_STEP + 1))
+        results = ctx.enter_context(tc.tile_pool(name="results", bufs=3))
         work = ctx.enter_context(tc.tile_pool(name="work", bufs=2))
         keep_v = ctx.enter_context(tc.tile_pool(name="keep_v", bufs=3))
         small = ctx.enter_context(tc.tile_pool(name="small", bufs=3))
@@ -58,17 +58,6 @@ def tile_relativeattentionhead_pa_t_kernel(tc, x, q, k, Wv, rel_emb, out):
 
         ident_f32 = const.tile([P, P], F32)
         make_identity(nc, ident_f32[:])
-        ident_bf16 = const.tile([P, P], BF16)
-        make_identity(nc, ident_bf16[:])
-
-        causal_f32 = const.tile([P, P], F32)
-        nc.gpsimd.memset(causal_f32[:], 0.0)
-        nc.gpsimd.affine_select(
-            out=causal_f32[:], in_=causal_f32[:], pattern=[[-1, P]], compare_op=ALU.is_ge, fill=MASKED,
-            base=0, channel_multiplier=1,
-        )
-        causal = const.tile([P, P], BF16)
-        nc.vector.tensor_copy(out=causal[:], in_=causal_f32[:])
 
         rel_rows = [const.tile([P, SKEW_PITCH], F32, name="rel_rows%d" % j) for j in range(N_SLOTS)]
         for j in range(N_SLOTS):
@@ -94,15 +83,12 @@ def tile_relativeattentionhead_pa_t_kernel(tc, x, q, k, Wv, rel_emb, out):
             )
             return raw
 
-        def head_to_partitions(raw, words):
+        def head_to_partitions(raw, words, copy):
             raw_words = raw[:].bitcast(F32)
             turned = psum.tile([P, NT, P], F32, tag="bank")
             for t in range(NT):
                 nc.tensor.transpose(turned[:, t, :], raw_words[:, t * P : (t + 1) * P], ident_f32[:])
-            nc.scalar.copy(
-                out=words[:].rearrange("w (p t) -> w p t", t=NT),
-                in_=turned[:].rearrange("w t p -> w p t"),
-            )
+            copy(out=words[:].rearrange("w (p t) -> w p t", t=NT), in_=turned[:].rearrange("w t p -> w p t"))
 
         def halves(words):
             return words[:].bitcast(BF16).rearrange("w (r h) -> w r h", h=2)
@@ -119,50 +105,53 @@ def tile_relativeattentionhead_pa_t_kernel(tc, x, q, k, Wv, rel_emb, out):
 
         q_raw, k_raw, x_raw = {}, {}, {}
         q_t, k_t, rel_skewed = {}, {}, {}
+        rel_words = const.tile([P, L], F32)
+        rel_t = halves(rel_words)
         x_grouped, x_codes, x_scales, v_grouped, v_codes, v_scales = {}, {}, {}, {}, {}, {}
         neg_max, row_sum, e_grouped, e_codes, e_scales, result = {}, {}, {}, {}, {}, {}
 
-        def load(b_qk, b_x):
-            if 0 <= b_qk < B:
-                q_raw[b_qk] = load_rows(raw_qk, q[b_qk], NT)
-                k_raw[b_qk] = load_rows(raw_qk, k[b_qk], NT)
-            if 0 <= b_x < B:
-                x_raw[b_x] = load_blocks(raw_x, x[b_x], 2, 2)
+        def load_q(b):
+            if b < B:
+                q_raw[b] = load_rows(raw_qk, q[b], NT)
 
-        rel_raw = load_rows(raw_qk, rel_emb, NT)
-        load(0, -1)
-        w_raw = load_blocks(raw_x, Wv, H // P, 1)
+        def load_k(b):
+            if b < B:
+                k_raw[b] = load_rows(raw_qk, k[b], NT)
 
-        rel_words = const.tile([P, L], F32)
-        head_to_partitions(rel_raw, rel_words)
-        rel_t = halves(rel_words)
+        def load_x(b):
+            if b < B:
+                x_raw[b] = load_blocks(raw_x, x[b], 2, 2)
 
-        w_grouped = const.tile([P, X_PASSES * H * 4], BF16, align_bytes=64)
-        for g in range(X_PASSES):
-            features_to_partitions(w_raw, H // P, w_grouped, g, 0, nc.vector.tensor_copy)
-        w_codes = const.tile([P, X_PASSES * H], U32, align_bytes=64)
-        w_scales = const.tile([P, X_PASSES * H], U8, align_bytes=64)
-        nc.vector.quantize_mx(out=w_codes[:].bitcast(FP8X4), scales=w_scales[:], in_=w_grouped[:])
+        def transpose_q(b, copy):
+            words = heads.tile([P, L], F32, tag="q_words")
+            head_to_partitions(q_raw[b], words, copy)
+            q_t[b] = halves(words)
 
-        def q_times(acc, b, i, other, cols, masked):
+        def transpose_k(b, copy):
+            words = heads.tile([P, L], F32, tag="k_words")
+            head_to_partitions(k_raw[b], words, copy)
+            k_t[b] = halves(words)
+
+        def transpose_x(b, r):
+            if r == 0:
+                x_grouped[b] = work.tile([P, L * X_PASSES * 4], BF16, align_bytes=64, name="x_grouped")
+            copy = nc.vector.tensor_copy if r < 2 else nc.scalar.copy
+            features_to_partitions(x_raw[b], NT, x_grouped[b], r // 2, r % 2, copy)
+
+        def q_times(acc, b, i, other, cols):
             for h in range(2):
                 nc.tensor.matmul(
-                    out=acc, lhsT=q_t[b][:, i * P : (i + 1) * P, h], rhs=other[:, cols, h],
-                    start=(h == 0), stop=(h == 1 and not masked),
+                    out=acc, lhsT=q_t[b][:, i * P : (i + 1) * P, h], rhs=other[:, cols, h], start=(h == 0), stop=(h == 1)
                 )
-            if masked:
-                nc.tensor.matmul(out=acc, lhsT=ident_bf16[:], rhs=causal[:], start=False, stop=True)
 
         def q_times_k(b, i):
             acc = psum.tile([P, L], F32, tag="bank")
-            if i > 0:
-                q_times(acc[:, 0 : i * P], b, i, k_t[b], slice(0, i * P), False)
-            q_times(acc[:, i * P : (i + 1) * P], b, i, k_t[b], slice(i * P, (i + 1) * P), True)
+            q_times(acc[:, 0 : ROW_W[i]], b, i, k_t[b], slice(0, ROW_W[i]))
             return acc
 
         def q_times_rel(b, i):
             acc = psum.tile([P, L], F32, tag="bank")
-            q_times(acc[:, 0 : ROW_W[i]], b, i, rel_t, slice(L - ROW_W[i], L), False)
+            q_times(acc[:, 0 : ROW_W[i]], b, i, rel_t, slice(L - ROW_W[i], L))
             return acc
 
         def negated_scores(b, i, acc):
@@ -182,9 +171,9 @@ def tile_relativeattentionhead_pa_t_kernel(tc, x, q, k, Wv, rel_emb, out):
                 scale=-1.0, accum_out=row_sum[b][:, i : i + 1],
             )
 
-        def park_relative_rows(b, i, acc):
+        def park_relative_rows(b, i, acc, copy):
             rows = rel_rows[(B - 1 - b) % N_SLOTS]
-            nc.scalar.copy(out=rows[:, ROW_OFF[i] : ROW_OFF[i] + ROW_W[i]], in_=acc[:, 0 : ROW_W[i]])
+            copy(out=rows[:, ROW_OFF[i] : ROW_OFF[i] + ROW_W[i]], in_=acc[:, 0 : ROW_W[i]])
 
         def send_rows(b):
             start = slot_start(b)
@@ -198,6 +187,12 @@ def tile_relativeattentionhead_pa_t_kernel(tc, x, q, k, Wv, rel_emb, out):
             shifted = out_flat[start : start + P * (SKEW_PITCH - 1)].rearrange("(a u) -> a u", u=SKEW_PITCH - 1)
             rel_skewed[b] = skewed.tile([P, ROW_COLS], F32, name="rel_skewed")
             nc.sync.dma_start(out=rel_skewed[b][:], in_=shifted[:, 0:ROW_COLS])
+            for i in reversed(range(NT)):
+                diagonal = rel_skewed[b][:, ROW_OFF[i] + i * P : ROW_OFF[i] + ROW_W[i]]
+                nc.gpsimd.affine_select(
+                    out=diagonal, in_=diagonal, pattern=[[-1, P]], compare_op=ALU.is_ge, fill=MASKED, base=0,
+                    channel_multiplier=1,
+                )
 
         def transpose_e(b, first):
             words = e_rows[b % 2][:].bitcast(F32)
@@ -211,44 +206,36 @@ def tile_relativeattentionhead_pa_t_kernel(tc, x, q, k, Wv, rel_emb, out):
             nc.scalar.copy(out=dest[:, first : first + 2, :, :], in_=turned[:].rearrange("p i u a -> p i a u"))
 
         def matmuls_and_transposes(n):
-            b_e, b_rel, b_x, b_qk = n - 1, n + LEAD, n + 2, n + LEAD + 1
-            if 0 <= n < B:
+            b_e, b_rel, b_x, b_q, b_k = n - 1, n + LEAD, n + 1, n + LEAD + 1, n + 1
+            if n < B:
                 neg_max[n] = small.tile([P, NT], F32, name="neg_max")
                 row_sum[n] = small.tile([P, NT], F32, name="row_sum")
-            if 0 <= b_e < B:
+            if b_e >= 0:
                 e_grouped[b_e] = work.tile([P, L * NT], BF16, align_bytes=64, name="e_grouped")
-            if 0 <= b_x < B:
-                x_grouped[b_x] = work.tile([P, L * X_PASSES * 4], BF16, align_bytes=64, name="x_grouped")
             for r in range(NT):
                 i = NT - 1 - r
-                if 0 <= n < B:
+                if n < B:
                     acc_k = q_times_k(n, i)
-                if 0 <= b_e < B and r % 2 == 0:
+                if b_e >= 0 and r % 2 == 0:
                     transpose_e(b_e, 2 - r)
-                if 0 <= b_rel < B:
-                    park_relative_rows(b_rel, i, q_times_rel(b_rel, i))
-                if 0 <= n < B:
+                if b_rel < B:
+                    park_relative_rows(b_rel, i, q_times_rel(b_rel, i), nc.scalar.copy)
+                if n < B:
                     negated_scores(n, i, acc_k)
                     if r >= 1:
                         negated_maximum(n, i + 1)
                     if r >= 2:
                         softmax_numerators(n, i + 2)
-                if 0 <= b_x < B:
-                    copy = nc.vector.tensor_copy if r < 2 else nc.scalar.copy
-                    features_to_partitions(x_raw[b_x], NT, x_grouped[b_x], r // 2, r % 2, copy)
-                if 0 <= b_qk < B and r < 2:
-                    words = heads.tile([P, L], F32, tag="q_words" if r == 0 else "k_words")
-                    head_to_partitions(q_raw[b_qk] if r == 0 else k_raw[b_qk], words)
-                    if r == 0:
-                        q_t[b_qk] = halves(words)
-                    else:
-                        k_t[b_qk] = halves(words)
-            if 0 <= n < B:
+                if b_x < B:
+                    transpose_x(b_x, r)
+                if b_k < B and r == 1:
+                    transpose_k(b_k, nc.scalar.copy)
+                if b_q < B and r == 2:
+                    transpose_q(b_q, nc.scalar.copy)
+            if n < B:
                 negated_maximum(n, 0)
                 softmax_numerators(n, 1)
                 softmax_numerators(n, 0)
-            if 0 <= b_rel < B:
-                send_rows(b_rel)
 
         def quantise(pool, grouped, name):
             n_words = grouped.shape[1] // 4
@@ -298,25 +285,66 @@ def tile_relativeattentionhead_pa_t_kernel(tc, x, q, k, Wv, rel_emb, out):
                 )
 
         with tc.manual_schedule():
-            for n in range(-(LEAD + 2), B + 1):
-                if 0 <= n + LEAD - 1 < B:
-                    fetch_skewed(n + LEAD - 1)
-                matmuls_and_transposes(n)
-                load(n + LEAD + 3, n + 4)
+            rel_raw = load_rows(raw_qk, rel_emb, NT)
+            load_q(0)
+            load_q(1)
+            w_raw = load_blocks(raw_x, Wv, H // P, 1)
+            load_k(0)
+            load_x(0)
 
-                if 0 <= n - 1 < B:
+            head_to_partitions(rel_raw, rel_words, nc.scalar.copy)
+            transpose_q(0, nc.vector.tensor_copy)
+            for i in reversed(range(NT)):
+                park_relative_rows(0, i, q_times_rel(0, i), nc.scalar.copy if i % 2 == 1 else nc.vector.tensor_copy)
+                if i == NT - 1:
+                    transpose_q(1, nc.vector.tensor_copy)
+            send_rows(0)
+            load_x(1)
+            load_q(2)
+            fetch_skewed(0)
+            w_grouped = const.tile([P, X_PASSES * H * 4], BF16, align_bytes=64)
+            for g in range(X_PASSES):
+                features_to_partitions(w_raw, H // P, w_grouped, g, 0, nc.vector.tensor_copy)
+            transpose_k(0, nc.scalar.copy)
+            for i in reversed(range(NT)):
+                park_relative_rows(1, i, q_times_rel(1, i), nc.scalar.copy if i % 2 == 1 else nc.vector.tensor_copy)
+            send_rows(1)
+            load_k(1)
+            load_q(3)
+            w_codes = const.tile([P, X_PASSES * H], U32, align_bytes=64)
+            w_scales = const.tile([P, X_PASSES * H], U8, align_bytes=64)
+            nc.vector.quantize_mx(out=w_codes[:].bitcast(FP8X4), scales=w_scales[:], in_=w_grouped[:])
+            for r in range(NT):
+                transpose_x(0, r)
+            transpose_q(2, nc.scalar.copy)
+            x_codes[0], x_scales[0] = quantise(work, x_grouped[0][:], "x")
+            for n in range(B + 1):
+                if n + LEAD - 1 < B:
+                    fetch_skewed(n + LEAD - 1)
+                if n == 0:
+                    load_x(2)
+                    load_q(4)
+                    load_k(2)
+                matmuls_and_transposes(n)
+                if n + LEAD < B:
+                    send_rows(n + LEAD)
+                load_x(n + 3)
+                load_q(n + 5)
+                load_k(n + 3)
+
+                if n >= 1:
                     inv_sum = small.tile([P, NT], F32)
                     nc.vector.reciprocal(out=inv_sum[:], in_=row_sum[n - 1][:])
                     e_codes[n - 1], e_scales[n - 1] = quantise(work, e_grouped[n - 1][:], "e")
-                if 0 <= n < B:
-                    v_codes[n], v_scales[n] = quantise(keep_v, v_grouped[n][:].rearrange("p c t -> p (c t)"), "v")
-                if 0 <= n + 2 < B:
-                    x_codes[n + 2], x_scales[n + 2] = quantise(work, x_grouped[n + 2][:], "x")
+                    v_codes[n - 1], v_scales[n - 1] = quantise(
+                        keep_v, v_grouped[n - 1][:].rearrange("p c t -> p (c t)"), "v"
+                    )
+                if n + 1 < B:
+                    x_codes[n + 1], x_scales[n + 1] = quantise(work, x_grouped[n + 1][:], "x")
 
-                if 0 <= n + 1 < B:
-                    project_v(n + 1)
-                if 0 <= n - 1 < B:
+                if n < B:
+                    project_v(n)
+                if n >= 1:
                     weighted_sum(n - 1, inv_sum)
-                if n >= FIRST_STORE_STEP:
-                    for b in range(0 if n == FIRST_STORE_STEP else n - 1, n):
-                        nc.sync.dma_start(out=out[b].rearrange("(i a) h -> a i h", a=P), in_=result[b][:])
+                if n >= 1:
+                    nc.sync.dma_start(out=out[n - 1].rearrange("(i a) h -> a i h", a=P), in_=result[n - 1][:])

@@ -30,6 +30,7 @@ SKEW_PAD = 8
 SKEW_PITCH = ROW_COLS + SKEW_PAD
 SLOT = P * SKEW_PITCH
 N_SLOTS = 2
+LAST_LOAD_STEP = B - 3
 LEAD = 2
 assert N_SLOTS * SLOT <= LEAD * L * H + L * H
 
@@ -50,11 +51,12 @@ def tile_relativeattentionhead_pa_t_kernel(tc, x, q, k, Wv, rel_emb, out):
         raw_qk = ctx.enter_context(tc.tile_pool(name="raw_qk", bufs=8))
         heads = ctx.enter_context(tc.tile_pool(name="heads", bufs=LEAD + 2))
         skewed = ctx.enter_context(tc.tile_pool(name="skewed", bufs=LEAD + 1))
-        results = ctx.enter_context(tc.tile_pool(name="results", bufs=3))
+        results = ctx.enter_context(tc.tile_pool(name="results", bufs=11))
         work = ctx.enter_context(tc.tile_pool(name="work", bufs=2))
         keep_v = ctx.enter_context(tc.tile_pool(name="keep_v", bufs=3))
         small = ctx.enter_context(tc.tile_pool(name="small", bufs=3))
-        psum = ctx.enter_context(tc.psum_pool(name="psum", bufs=8))
+        psum = ctx.enter_context(tc.psum_pool(name="psum", bufs=7))
+        psum_low = ctx.enter_context(tc.psum_pool(name="psum_low", bufs=1))
 
         ident_f32 = const.tile([P, P], F32)
         make_identity(nc, ident_f32[:])
@@ -68,6 +70,9 @@ def tile_relativeattentionhead_pa_t_kernel(tc, x, q, k, Wv, rel_emb, out):
             nc.vector.memset(e_rows[j][:].bitcast(I32), 0)
         zeros = const.tile([P, P], F32)
         nc.vector.memset(zeros[:], 0.0)
+        turned_low = psum_low.tile([P, 2, 2, P], F32)
+        for j in range(2):
+            nc.tensor.transpose(turned_low[:, j, 1, :], zeros[:], ident_f32[:])
 
         def load_rows(pool, rows, per_partition):
             raw = pool.tile([P, per_partition * rows.shape[1]], BF16, tag="raw")
@@ -135,7 +140,7 @@ def tile_relativeattentionhead_pa_t_kernel(tc, x, q, k, Wv, rel_emb, out):
         def transpose_x(b, r):
             if r == 0:
                 x_grouped[b] = work.tile([P, L * X_PASSES * 4], BF16, align_bytes=64, name="x_grouped")
-            copy = nc.vector.tensor_copy if r < 2 else nc.scalar.copy
+            copy = nc.scalar.copy if r < 2 else nc.vector.tensor_copy
             features_to_partitions(x_raw[b], NT, x_grouped[b], r // 2, r % 2, copy)
 
         def q_times(acc, b, i, other, cols):
@@ -196,14 +201,20 @@ def tile_relativeattentionhead_pa_t_kernel(tc, x, q, k, Wv, rel_emb, out):
 
         def transpose_e(b, first):
             words = e_rows[b % 2][:].bitcast(F32)
-            turned = psum.tile([P, 2, 2, P], F32, tag="bank")
+            turned = turned_low if first == 0 else psum.tile([P, 2, 2, P], F32, tag="bank")
             for j in range(2):
-                for u in range(2):
+                for u in range(E_W[first + j] // (2 * P)):
                     col = (E_OFF[first + j] + 2 * P * u) // 2
-                    block = words[:, col : col + P] if 2 * P * u < E_W[first + j] else zeros[:]
-                    nc.tensor.transpose(turned[:, j, u, :], block, ident_f32[:])
+                    nc.tensor.transpose(turned[:, j, u, :], words[:, col : col + P], ident_f32[:])
             dest = e_grouped[b][:].bitcast(F32).rearrange("p (i a u) -> p i a u", i=NT, u=2)
             nc.scalar.copy(out=dest[:, first : first + 2, :, :], in_=turned[:].rearrange("p i u a -> p i a u"))
+
+        def quantise(pool, grouped, name):
+            n_words = grouped.shape[1] // 4
+            codes = pool.tile([P, n_words], U32, align_bytes=64, name=name + "_codes")
+            scales = pool.tile([P, n_words], U8, align_bytes=64, name=name + "_scales")
+            nc.vector.quantize_mx(out=codes[:].bitcast(FP8X4), scales=scales[:], in_=grouped)
+            return codes, scales
 
         def matmuls_and_transposes(n):
             b_e, b_rel, b_x, b_q, b_k = n - 1, n + LEAD, n + 1, n + LEAD + 1, n + 1
@@ -232,17 +243,14 @@ def tile_relativeattentionhead_pa_t_kernel(tc, x, q, k, Wv, rel_emb, out):
                     transpose_k(b_k, nc.scalar.copy)
                 if b_q < B and r == 2:
                     transpose_q(b_q, nc.scalar.copy)
+                if b_e >= 0 and r == 1:
+                    v_codes[b_e], v_scales[b_e] = quantise(keep_v, v_grouped[b_e][:].rearrange("p c t -> p (c t)"), "v")
+                if b_e >= 0 and r == 3:
+                    e_codes[b_e], e_scales[b_e] = quantise(work, e_grouped[b_e][:], "e")
             if n < B:
                 negated_maximum(n, 0)
                 softmax_numerators(n, 1)
                 softmax_numerators(n, 0)
-
-        def quantise(pool, grouped, name):
-            n_words = grouped.shape[1] // 4
-            codes = pool.tile([P, n_words], U32, align_bytes=64, name=name + "_codes")
-            scales = pool.tile([P, n_words], U8, align_bytes=64, name=name + "_scales")
-            nc.vector.quantize_mx(out=codes[:].bitcast(FP8X4), scales=scales[:], in_=grouped)
-            return codes, scales
 
         def project_v(b):
             v_grouped[b] = work.tile([P, H, NT], BF16, align_bytes=64, name="v_grouped")
@@ -288,41 +296,43 @@ def tile_relativeattentionhead_pa_t_kernel(tc, x, q, k, Wv, rel_emb, out):
             rel_raw = load_rows(raw_qk, rel_emb, NT)
             load_q(0)
             load_q(1)
-            w_raw = load_blocks(raw_x, Wv, H // P, 1)
             load_k(0)
             load_x(0)
+            w_raw = load_blocks(raw_x, Wv, H // P, 1)
+            load_q(2)
 
             head_to_partitions(rel_raw, rel_words, nc.scalar.copy)
             transpose_q(0, nc.vector.tensor_copy)
-            for i in reversed(range(NT)):
-                park_relative_rows(0, i, q_times_rel(0, i), nc.scalar.copy if i % 2 == 1 else nc.vector.tensor_copy)
-                if i == NT - 1:
-                    transpose_q(1, nc.vector.tensor_copy)
-            send_rows(0)
-            load_x(1)
-            load_q(2)
-            fetch_skewed(0)
-            w_grouped = const.tile([P, X_PASSES * H * 4], BF16, align_bytes=64)
-            for g in range(X_PASSES):
-                features_to_partitions(w_raw, H // P, w_grouped, g, 0, nc.vector.tensor_copy)
-            transpose_k(0, nc.scalar.copy)
-            for i in reversed(range(NT)):
-                park_relative_rows(1, i, q_times_rel(1, i), nc.scalar.copy if i % 2 == 1 else nc.vector.tensor_copy)
-            send_rows(1)
+            for b in range(LEAD):
+                for i in reversed(range(NT)):
+                    park_relative_rows(b, i, q_times_rel(b, i), nc.scalar.copy if i % 2 == 1 else nc.vector.tensor_copy)
+                    if b == 0 and i == NT - 1:
+                        transpose_q(1, nc.vector.tensor_copy)
+                    if b == 1 and i == NT - 1:
+                        transpose_k(0, nc.scalar.copy)
+                send_rows(b)
+                if b == 0:
+                    load_x(1)
+                    fetch_skewed(0)
             load_k(1)
             load_q(3)
-            w_codes = const.tile([P, X_PASSES * H], U32, align_bytes=64)
-            w_scales = const.tile([P, X_PASSES * H], U8, align_bytes=64)
-            nc.vector.quantize_mx(out=w_codes[:].bitcast(FP8X4), scales=w_scales[:], in_=w_grouped[:])
             for r in range(NT):
                 transpose_x(0, r)
             transpose_q(2, nc.scalar.copy)
+            w_grouped = const.tile([P, X_PASSES * H * 4], BF16, align_bytes=64)
+            for g in range(X_PASSES):
+                features_to_partitions(w_raw, H // P, w_grouped, g, 0, nc.vector.tensor_copy)
+            w_codes = const.tile([P, X_PASSES * H], U32, align_bytes=64)
+            w_scales = const.tile([P, X_PASSES * H], U8, align_bytes=64)
             x_codes[0], x_scales[0] = quantise(work, x_grouped[0][:], "x")
+            nc.vector.quantize_mx(out=w_codes[:].bitcast(FP8X4), scales=w_scales[:], in_=w_grouped[:])
+            n_stored = 0
             for n in range(B + 1):
+                if n == 0:
+                    load_x(2)
                 if n + LEAD - 1 < B:
                     fetch_skewed(n + LEAD - 1)
                 if n == 0:
-                    load_x(2)
                     load_q(4)
                     load_k(2)
                 matmuls_and_transposes(n)
@@ -335,10 +345,6 @@ def tile_relativeattentionhead_pa_t_kernel(tc, x, q, k, Wv, rel_emb, out):
                 if n >= 1:
                     inv_sum = small.tile([P, NT], F32)
                     nc.vector.reciprocal(out=inv_sum[:], in_=row_sum[n - 1][:])
-                    e_codes[n - 1], e_scales[n - 1] = quantise(work, e_grouped[n - 1][:], "e")
-                    v_codes[n - 1], v_scales[n - 1] = quantise(
-                        keep_v, v_grouped[n - 1][:].rearrange("p c t -> p (c t)"), "v"
-                    )
                 if n + 1 < B:
                     x_codes[n + 1], x_scales[n + 1] = quantise(work, x_grouped[n + 1][:], "x")
 
@@ -346,5 +352,7 @@ def tile_relativeattentionhead_pa_t_kernel(tc, x, q, k, Wv, rel_emb, out):
                     project_v(n)
                 if n >= 1:
                     weighted_sum(n - 1, inv_sum)
-                if n >= 1:
-                    nc.sync.dma_start(out=out[n - 1].rearrange("(i a) h -> a i h", a=P), in_=result[n - 1][:])
+                n_due = n // 2 if n < LAST_LOAD_STEP else n // 2 + 2 if n < B - LEAD + 1 else n
+                for b in range(n_stored, n_due):
+                    nc.sync.dma_start(out=out[b].rearrange("(i a) h -> a i h", a=P), in_=result[b][:])
+                n_stored = n_due

@@ -19,9 +19,12 @@ K_PASS = 4 * P
 X_PASSES = E // K_PASS
 FLOPS = 2 * B * L * (E * H + 3 * L * H)
 
+GROUPS = ((3,), (2, 0), (1,))
 ROW_W = [P * (i + 1) for i in range(NT)]
-ROW_OFF = [sum(ROW_W[:i]) for i in range(NT)]
+ROW_ORDER = [i for group in GROUPS for i in group]
+ROW_OFF = [sum(ROW_W[j] for j in ROW_ORDER[: ROW_ORDER.index(i)]) for i in range(NT)]
 ROW_COLS = sum(ROW_W)
+
 E_W = [2 * P * (i // 2 + 1) for i in range(NT)]
 E_OFF = [sum(E_W[:i]) for i in range(NT)]
 E_COLS = sum(E_W)
@@ -29,10 +32,11 @@ E_COLS = sum(E_W)
 SKEW_PAD = 8
 SKEW_PITCH = ROW_COLS + SKEW_PAD
 SLOT = P * SKEW_PITCH
-N_SLOTS = 2
-LAST_LOAD_STEP = B - 3
-LEAD = 2
-assert N_SLOTS * SLOT <= LEAD * L * H + L * H
+N_SLOTS = 3
+LAST_LOAD_STEP = B - 4
+X_LEAD = 2
+LEAD = 3
+assert N_SLOTS * SLOT <= (LEAD + 1) * L * H
 
 MASKED = -(2.0**100)
 
@@ -53,7 +57,7 @@ def tile_relativeattentionhead_pa_t_kernel(tc, x, q, k, Wv, rel_emb, out):
         skewed = ctx.enter_context(tc.tile_pool(name="skewed", bufs=LEAD + 1))
         results = ctx.enter_context(tc.tile_pool(name="results", bufs=11))
         work = ctx.enter_context(tc.tile_pool(name="work", bufs=2))
-        keep_v = ctx.enter_context(tc.tile_pool(name="keep_v", bufs=3))
+        keep_v = ctx.enter_context(tc.tile_pool(name="keep_v", bufs=4))
         small = ctx.enter_context(tc.tile_pool(name="small", bufs=3))
         psum = ctx.enter_context(tc.psum_pool(name="psum", bufs=7))
         psum_low = ctx.enter_context(tc.psum_pool(name="psum_low", bufs=1))
@@ -140,7 +144,7 @@ def tile_relativeattentionhead_pa_t_kernel(tc, x, q, k, Wv, rel_emb, out):
         def transpose_x(b, r):
             if r == 0:
                 x_grouped[b] = work.tile([P, L * X_PASSES * 4], BF16, align_bytes=64, name="x_grouped")
-            copy = nc.scalar.copy if r < 2 else nc.vector.tensor_copy
+            copy = nc.scalar.copy if r < (2 if b < B - 1 else 3) else nc.vector.tensor_copy
             features_to_partitions(x_raw[b], NT, x_grouped[b], r // 2, r % 2, copy)
 
         def q_times(acc, b, i, other, cols):
@@ -149,20 +153,30 @@ def tile_relativeattentionhead_pa_t_kernel(tc, x, q, k, Wv, rel_emb, out):
                     out=acc, lhsT=q_t[b][:, i * P : (i + 1) * P, h], rhs=other[:, cols, h], start=(h == 0), stop=(h == 1)
                 )
 
-        def q_times_k(b, i):
+        def group_columns(group):
+            start = ROW_OFF[group[0]]
+            return slice(start, start + sum(ROW_W[i] for i in group))
+
+        def q_times_k(b, group):
             acc = psum.tile([P, L], F32, tag="bank")
-            q_times(acc[:, 0 : ROW_W[i]], b, i, k_t[b], slice(0, ROW_W[i]))
+            for i in group:
+                col = ROW_OFF[i] - ROW_OFF[group[0]]
+                q_times(acc[:, col : col + ROW_W[i]], b, i, k_t[b], slice(0, ROW_W[i]))
             return acc
 
-        def q_times_rel(b, i):
+        def q_times_rel(b, group):
             acc = psum.tile([P, L], F32, tag="bank")
-            q_times(acc[:, 0 : ROW_W[i]], b, i, rel_t, slice(L - ROW_W[i], L))
+            for i in group:
+                col = ROW_OFF[i] - ROW_OFF[group[0]]
+                q_times(acc[:, col : col + ROW_W[i]], b, i, rel_t, slice(L - ROW_W[i], L))
             return acc
 
-        def negated_scores(b, i, acc):
-            neg_s = rel_skewed[b][:, ROW_OFF[i] : ROW_OFF[i] + ROW_W[i]]
+        def negated_scores(b, group, acc):
+            cols = group_columns(group)
+            neg_s = rel_skewed[b][:, cols]
             nc.vector.scalar_tensor_tensor(
-                out=neg_s, in0=acc[:, 0 : ROW_W[i]], scalar=-1.0 / 16.0, in1=neg_s, op0=ALU.mult, op1=ALU.subtract
+                out=neg_s, in0=acc[:, 0 : cols.stop - cols.start], scalar=-1.0 / 16.0, in1=neg_s, op0=ALU.mult,
+                op1=ALU.subtract,
             )
 
         def negated_maximum(b, i):
@@ -176,9 +190,10 @@ def tile_relativeattentionhead_pa_t_kernel(tc, x, q, k, Wv, rel_emb, out):
                 scale=-1.0, accum_out=row_sum[b][:, i : i + 1],
             )
 
-        def park_relative_rows(b, i, acc, copy):
+        def park_relative_rows(b, group, acc, copy):
             rows = rel_rows[(B - 1 - b) % N_SLOTS]
-            copy(out=rows[:, ROW_OFF[i] : ROW_OFF[i] + ROW_W[i]], in_=acc[:, 0 : ROW_W[i]])
+            cols = group_columns(group)
+            copy(out=rows[:, cols], in_=acc[:, 0 : cols.stop - cols.start])
 
         def send_rows(b):
             start = slot_start(b)
@@ -192,7 +207,7 @@ def tile_relativeattentionhead_pa_t_kernel(tc, x, q, k, Wv, rel_emb, out):
             shifted = out_flat[start : start + P * (SKEW_PITCH - 1)].rearrange("(a u) -> a u", u=SKEW_PITCH - 1)
             rel_skewed[b] = skewed.tile([P, ROW_COLS], F32, name="rel_skewed")
             nc.sync.dma_start(out=rel_skewed[b][:], in_=shifted[:, 0:ROW_COLS])
-            for i in reversed(range(NT)):
+            for i in reversed(ROW_ORDER):
                 diagonal = rel_skewed[b][:, ROW_OFF[i] + i * P : ROW_OFF[i] + ROW_W[i]]
                 nc.gpsimd.affine_select(
                     out=diagonal, in_=diagonal, pattern=[[-1, P]], compare_op=ALU.is_ge, fill=MASKED, base=0,
@@ -217,40 +232,46 @@ def tile_relativeattentionhead_pa_t_kernel(tc, x, q, k, Wv, rel_emb, out):
             return codes, scales
 
         def matmuls_and_transposes(n):
-            b_e, b_rel, b_x, b_q, b_k = n - 1, n + LEAD, n + 1, n + LEAD + 1, n + 1
+            b_e, b_rel, b_x, b_q, b_k = n - 1, n + LEAD, n + X_LEAD, n + LEAD + 1, n + 1
+            b_v = n + X_LEAD - 2
             if n < B:
                 neg_max[n] = small.tile([P, NT], F32, name="neg_max")
                 row_sum[n] = small.tile([P, NT], F32, name="row_sum")
             if b_e >= 0:
                 e_grouped[b_e] = work.tile([P, L * NT], BF16, align_bytes=64, name="e_grouped")
-            for r in range(NT):
-                i = NT - 1 - r
+            for r, group in enumerate(GROUPS):
                 if n < B:
-                    acc_k = q_times_k(n, i)
-                if b_e >= 0 and r % 2 == 0:
+                    acc_k = q_times_k(n, group)
+                if b_e >= 0 and r != 1:
                     transpose_e(b_e, 2 - r)
                 if b_rel < B:
-                    park_relative_rows(b_rel, i, q_times_rel(b_rel, i), nc.scalar.copy)
+                    park_relative_rows(b_rel, group, q_times_rel(b_rel, group), nc.scalar.copy)
                 if n < B:
-                    negated_scores(n, i, acc_k)
+                    negated_scores(n, group, acc_k)
                     if r >= 1:
-                        negated_maximum(n, i + 1)
+                        for i in GROUPS[r - 1]:
+                            negated_maximum(n, i)
                     if r >= 2:
-                        softmax_numerators(n, i + 2)
+                        for i in GROUPS[r - 2]:
+                            softmax_numerators(n, i)
                 if b_x < B:
                     transpose_x(b_x, r)
                 if b_k < B and r == 1:
                     transpose_k(b_k, nc.scalar.copy)
+                if b_x < B and r == 2:
+                    transpose_x(b_x, 3)
                 if b_q < B and r == 2:
                     transpose_q(b_q, nc.scalar.copy)
-                if b_e >= 0 and r == 1:
-                    v_codes[b_e], v_scales[b_e] = quantise(keep_v, v_grouped[b_e][:].rearrange("p c t -> p (c t)"), "v")
-                if b_e >= 0 and r == 3:
+                if b_v < B and r == 1:
+                    v_codes[b_v], v_scales[b_v] = quantise(keep_v, v_grouped[b_v][:].rearrange("p c t -> p (c t)"), "v")
+                if b_e >= 0 and r == 2:
                     e_codes[b_e], e_scales[b_e] = quantise(work, e_grouped[b_e][:], "e")
             if n < B:
-                negated_maximum(n, 0)
-                softmax_numerators(n, 1)
-                softmax_numerators(n, 0)
+                for i in GROUPS[2]:
+                    negated_maximum(n, i)
+                for group in GROUPS[1:]:
+                    for i in group:
+                        softmax_numerators(n, i)
 
         def project_v(b):
             v_grouped[b] = work.tile([P, H, NT], BF16, align_bytes=64, name="v_grouped")
@@ -287,72 +308,89 @@ def tile_relativeattentionhead_pa_t_kernel(tc, x, q, k, Wv, rel_emb, out):
                         start=True,
                         stop=True,
                     )
-                nc.vector.tensor_tensor(
-                    out=result[b][:, tiles, :], in0=acc[:], in1=inv_sum[:, tiles].unsqueeze(2).to_broadcast([P, 2, H]),
-                    op=ALU.mult,
-                )
+                if pair == 0 and b + 1 + LEAD >= B:
+                    for j in range(2):
+                        i = 2 * pair + j
+                        nc.scalar.activation(
+                            out=result[b][:, i, :], in_=acc[:, j, :], func=ACT.Copy, scale=inv_sum[:, i : i + 1]
+                        )
+                else:
+                    nc.vector.tensor_tensor(
+                        out=result[b][:, tiles, :], in0=acc[:], in1=inv_sum[:, tiles].unsqueeze(2).to_broadcast([P, 2, H]),
+                        op=ALU.mult,
+                    )
 
         with tc.manual_schedule():
             rel_raw = load_rows(raw_qk, rel_emb, NT)
             load_q(0)
             load_q(1)
-            load_k(0)
             load_x(0)
-            w_raw = load_blocks(raw_x, Wv, H // P, 1)
             load_q(2)
+            w_raw = load_blocks(raw_x, Wv, H // P, 1)
 
             head_to_partitions(rel_raw, rel_words, nc.scalar.copy)
             transpose_q(0, nc.vector.tensor_copy)
-            for b in range(LEAD):
-                for i in reversed(range(NT)):
-                    park_relative_rows(b, i, q_times_rel(b, i), nc.scalar.copy if i % 2 == 1 else nc.vector.tensor_copy)
-                    if b == 0 and i == NT - 1:
-                        transpose_q(1, nc.vector.tensor_copy)
-                    if b == 1 and i == NT - 1:
-                        transpose_k(0, nc.scalar.copy)
+
+            def relative_term(b):
+                for r, group in enumerate(GROUPS):
+                    park_relative_rows(b, group, q_times_rel(b, group), nc.vector.tensor_copy if r == 1 else nc.scalar.copy)
                 send_rows(b)
-                if b == 0:
-                    load_x(1)
-                    fetch_skewed(0)
-            load_k(1)
+
+            relative_term(0)
+            load_x(1)
             load_q(3)
+            load_k(0)
+            transpose_q(1, nc.vector.tensor_copy)
             for r in range(NT):
                 transpose_x(0, r)
-            transpose_q(2, nc.scalar.copy)
+            relative_term(1)
+            fetch_skewed(0)
+            load_x(2)
+            transpose_q(2, nc.vector.tensor_copy)
+            x_codes[0], x_scales[0] = quantise(work, x_grouped[0][:], "x")
             w_grouped = const.tile([P, X_PASSES * H * 4], BF16, align_bytes=64)
             for g in range(X_PASSES):
                 features_to_partitions(w_raw, H // P, w_grouped, g, 0, nc.vector.tensor_copy)
             w_codes = const.tile([P, X_PASSES * H], U32, align_bytes=64)
             w_scales = const.tile([P, X_PASSES * H], U8, align_bytes=64)
-            x_codes[0], x_scales[0] = quantise(work, x_grouped[0][:], "x")
             nc.vector.quantize_mx(out=w_codes[:].bitcast(FP8X4), scales=w_scales[:], in_=w_grouped[:])
+            relative_term(2)
+            load_k(1)
+            load_q(4)
+            for r in range(NT):
+                transpose_x(1, r)
+            transpose_k(0, nc.scalar.copy)
+            transpose_q(3, nc.scalar.copy)
+            x_codes[1], x_scales[1] = quantise(work, x_grouped[1][:], "x")
+            project_v(0)
+            fetch_skewed(1)
+            load_k(2)
+            load_x(3)
+            load_q(5)
+
             n_stored = 0
             for n in range(B + 1):
-                if n == 0:
-                    load_x(2)
                 if n + LEAD - 1 < B:
                     fetch_skewed(n + LEAD - 1)
-                if n == 0:
-                    load_q(4)
-                    load_k(2)
                 matmuls_and_transposes(n)
                 if n + LEAD < B:
                     send_rows(n + LEAD)
-                load_x(n + 3)
-                load_q(n + 5)
+                load_q(n + LEAD + 3)
                 load_k(n + 3)
+                load_x(n + X_LEAD + 2)
 
                 if n >= 1:
                     inv_sum = small.tile([P, NT], F32)
                     nc.vector.reciprocal(out=inv_sum[:], in_=row_sum[n - 1][:])
-                if n + 1 < B:
-                    x_codes[n + 1], x_scales[n + 1] = quantise(work, x_grouped[n + 1][:], "x")
-
-                if n < B:
-                    project_v(n)
+                if n + X_LEAD < B:
+                    x_codes[n + X_LEAD], x_scales[n + X_LEAD] = quantise(work, x_grouped[n + X_LEAD][:], "x")
+                if n + X_LEAD - 1 < B:
+                    project_v(n + X_LEAD - 1)
                 if n >= 1:
                     weighted_sum(n - 1, inv_sum)
                 n_due = n // 2 if n < LAST_LOAD_STEP else n // 2 + 2 if n < B - LEAD + 1 else n
                 for b in range(n_stored, n_due):
-                    nc.sync.dma_start(out=out[b].rearrange("(i a) h -> a i h", a=P), in_=result[b][:])
+                    rows = out[b].rearrange("(i a) h -> a i h", a=P)
+                    for tiles in (slice(0, 2), slice(2, 4)) if b == B - 1 else (slice(0, 4),):
+                        nc.sync.dma_start(out=rows[:, tiles, :], in_=result[b][:, tiles, :])
                 n_stored = n_due

@@ -62,6 +62,12 @@ def tile_relativeattentionhead_pa_t_kernel(tc, x, q, k, Wv, rel_emb, out):
         psum = ctx.enter_context(tc.psum_pool(name="psum", bufs=7))
         psum_low = ctx.enter_context(tc.psum_pool(name="psum_low", bufs=1))
 
+        zeros = const.tile([P, L], BF16)
+        nc.vector.memset(zeros[:].bitcast(I32), 0)
+        idle = psum.tile([P, L], F32, tag="bank")
+        for i in range(4):
+            nc.tensor.matmul(out=idle[:], lhsT=zeros[:, 0:P], rhs=zeros[:], start=True, stop=True)
+
         ident_f32 = const.tile([P, P], F32)
         make_identity(nc, ident_f32[:])
 
@@ -72,11 +78,9 @@ def tile_relativeattentionhead_pa_t_kernel(tc, x, q, k, Wv, rel_emb, out):
         e_rows = [const.tile([P, E_COLS], BF16, name="e_rows%d" % j) for j in range(2)]
         for j in range(2):
             nc.vector.memset(e_rows[j][:].bitcast(I32), 0)
-        zeros = const.tile([P, P], F32)
-        nc.vector.memset(zeros[:], 0.0)
         turned_low = psum_low.tile([P, 2, 2, P], F32)
         for j in range(2):
-            nc.tensor.transpose(turned_low[:, j, 1, :], zeros[:], ident_f32[:])
+            nc.tensor.transpose(turned_low[:, j, 1, :], zeros[:].bitcast(F32)[:, 0:P], ident_f32[:])
 
         def load_rows(pool, rows, per_partition):
             raw = pool.tile([P, per_partition * rows.shape[1]], BF16, tag="raw")
@@ -214,7 +218,7 @@ def tile_relativeattentionhead_pa_t_kernel(tc, x, q, k, Wv, rel_emb, out):
                     channel_multiplier=1,
                 )
 
-        def transpose_e(b, first):
+        def transpose_e(b, first, copy):
             words = e_rows[b % 2][:].bitcast(F32)
             turned = turned_low if first == 0 else psum.tile([P, 2, 2, P], F32, tag="bank")
             for j in range(2):
@@ -222,7 +226,7 @@ def tile_relativeattentionhead_pa_t_kernel(tc, x, q, k, Wv, rel_emb, out):
                     col = (E_OFF[first + j] + 2 * P * u) // 2
                     nc.tensor.transpose(turned[:, j, u, :], words[:, col : col + P], ident_f32[:])
             dest = e_grouped[b][:].bitcast(F32).rearrange("p (i a u) -> p i a u", i=NT, u=2)
-            nc.scalar.copy(out=dest[:, first : first + 2, :, :], in_=turned[:].rearrange("p i u a -> p i a u"))
+            copy(out=dest[:, first : first + 2, :, :], in_=turned[:].rearrange("p i u a -> p i a u"))
 
         def quantise(pool, grouped, name):
             n_words = grouped.shape[1] // 4
@@ -230,6 +234,16 @@ def tile_relativeattentionhead_pa_t_kernel(tc, x, q, k, Wv, rel_emb, out):
             scales = pool.tile([P, n_words], U8, align_bytes=64, name=name + "_scales")
             nc.vector.quantize_mx(out=codes[:].bitcast(FP8X4), scales=scales[:], in_=grouped)
             return codes, scales
+
+        def quantise_e(b, tiles):
+            if b not in e_codes:
+                e_codes[b] = work.tile([P, L], U32, align_bytes=64, name="e_codes")
+                e_scales[b] = work.tile([P, L], U8, align_bytes=64, name="e_scales")
+            cols = slice(tiles.start * P, tiles.stop * P)
+            nc.vector.quantize_mx(
+                out=e_codes[b][:, cols].bitcast(FP8X4), scales=e_scales[b][:, cols],
+                in_=e_grouped[b][:, tiles.start * P * NT : tiles.stop * P * NT],
+            )
 
         def matmuls_and_transposes(n):
             b_e, b_rel, b_x, b_q, b_k = n - 1, n + LEAD, n + X_LEAD, n + LEAD + 1, n + 1
@@ -243,7 +257,7 @@ def tile_relativeattentionhead_pa_t_kernel(tc, x, q, k, Wv, rel_emb, out):
                 if n < B:
                     acc_k = q_times_k(n, group)
                 if b_e >= 0 and r != 1:
-                    transpose_e(b_e, 2 - r)
+                    transpose_e(b_e, 2 - r, nc.vector.tensor_copy if b_e == B - 1 and r == 0 else nc.scalar.copy)
                 if b_rel < B:
                     park_relative_rows(b_rel, group, q_times_rel(b_rel, group), nc.scalar.copy)
                 if n < B:
@@ -264,8 +278,10 @@ def tile_relativeattentionhead_pa_t_kernel(tc, x, q, k, Wv, rel_emb, out):
                     transpose_q(b_q, nc.scalar.copy)
                 if b_v < B and r == 1:
                     v_codes[b_v], v_scales[b_v] = quantise(keep_v, v_grouped[b_v][:].rearrange("p c t -> p (c t)"), "v")
-                if b_e >= 0 and r == 2:
-                    e_codes[b_e], e_scales[b_e] = quantise(work, e_grouped[b_e][:], "e")
+                if b_e == B - 1 and r != 1:
+                    quantise_e(b_e, slice(2 - r, 4 - r))
+                elif b_e >= 0 and r == 2:
+                    quantise_e(b_e, slice(0, NT))
             if n < B:
                 for i in GROUPS[2]:
                     negated_maximum(n, i)
@@ -294,7 +310,7 @@ def tile_relativeattentionhead_pa_t_kernel(tc, x, q, k, Wv, rel_emb, out):
 
         def weighted_sum(b, inv_sum):
             result[b] = results.tile([P, NT, H], F32, name="result")
-            for pair in range(NT // 2):
+            for pair in reversed(range(NT // 2)):
                 tiles = slice(2 * pair, 2 * pair + 2)
                 acc = psum.tile([P, 2, H], F32, tag="bank")
                 for j in range(2):
@@ -391,6 +407,6 @@ def tile_relativeattentionhead_pa_t_kernel(tc, x, q, k, Wv, rel_emb, out):
                 n_due = n // 2 if n < LAST_LOAD_STEP else n // 2 + 2 if n < B - LEAD + 1 else n
                 for b in range(n_stored, n_due):
                     rows = out[b].rearrange("(i a) h -> a i h", a=P)
-                    for tiles in (slice(0, 2), slice(2, 4)) if b == B - 1 else (slice(0, 4),):
+                    for tiles in (slice(2, 4), slice(0, 2)) if b == B - 1 else (slice(0, 4),):
                         nc.sync.dma_start(out=rows[:, tiles, :], in_=result[b][:, tiles, :])
                 n_stored = n_due

@@ -33,7 +33,6 @@ SKEW_PAD = 8
 SKEW_PITCH = ROW_COLS + SKEW_PAD
 SLOT = P * SKEW_PITCH
 N_SLOTS = 3
-LAST_LOAD_STEP = B - 4
 X_LEAD = 2
 LEAD = 3
 assert N_SLOTS * SLOT <= (LEAD + 1) * L * H
@@ -211,11 +210,12 @@ def tile_relativeattentionhead_pa_t_kernel(tc, x, q, k, Wv, rel_emb, out):
             shifted = out_flat[start : start + P * (SKEW_PITCH - 1)].rearrange("(a u) -> a u", u=SKEW_PITCH - 1)
             rel_skewed[b] = skewed.tile([P, ROW_COLS], F32, name="rel_skewed")
             nc.sync.dma_start(out=rel_skewed[b][:], in_=shifted[:, 0:ROW_COLS])
-            for i in reversed(ROW_ORDER):
-                diagonal = rel_skewed[b][:, ROW_OFF[i] + i * P : ROW_OFF[i] + ROW_W[i]]
+            diagonals = [(ROW_OFF[group[0]] + group[0] * P, len(group)) for group in GROUPS]
+            for start, n_tiles in diagonals if b == 0 else reversed(diagonals):
+                diagonal = rel_skewed[b][:, start : start + n_tiles * P]
                 nc.gpsimd.affine_select(
-                    out=diagonal, in_=diagonal, pattern=[[-1, P]], compare_op=ALU.is_ge, fill=MASKED, base=0,
-                    channel_multiplier=1,
+                    out=diagonal, in_=diagonal, pattern=[[0, n_tiles], [-1, P]], compare_op=ALU.is_ge, fill=MASKED,
+                    base=0, channel_multiplier=1,
                 )
 
         def transpose_e(b, first, copy):
@@ -268,12 +268,10 @@ def tile_relativeattentionhead_pa_t_kernel(tc, x, q, k, Wv, rel_emb, out):
                     if r >= 2:
                         for i in GROUPS[r - 2]:
                             softmax_numerators(n, i)
-                if b_x < B:
-                    transpose_x(b_x, r)
-                if b_k < B and r == 1:
+                for j in ((), (0, 1), (2, 3))[r] if b_x < B else ():
+                    transpose_x(b_x, j)
+                if b_k < B and r == 0:
                     transpose_k(b_k, nc.scalar.copy)
-                if b_x < B and r == 2:
-                    transpose_x(b_x, 3)
                 if b_q < B and r == 2:
                     transpose_q(b_q, nc.scalar.copy)
                 if b_v < B and r == 1:
@@ -356,6 +354,7 @@ def tile_relativeattentionhead_pa_t_kernel(tc, x, q, k, Wv, rel_emb, out):
             load_x(1)
             load_q(3)
             load_k(0)
+            load_k(1)
             transpose_q(1, nc.vector.tensor_copy)
             for r in range(NT):
                 transpose_x(0, r)
@@ -371,7 +370,6 @@ def tile_relativeattentionhead_pa_t_kernel(tc, x, q, k, Wv, rel_emb, out):
             w_scales = const.tile([P, X_PASSES * H], U8, align_bytes=64)
             nc.vector.quantize_mx(out=w_codes[:].bitcast(FP8X4), scales=w_scales[:], in_=w_grouped[:])
             relative_term(2)
-            load_k(1)
             load_q(4)
             for r in range(NT):
                 transpose_x(1, r)
@@ -404,7 +402,7 @@ def tile_relativeattentionhead_pa_t_kernel(tc, x, q, k, Wv, rel_emb, out):
                     project_v(n + X_LEAD - 1)
                 if n >= 1:
                     weighted_sum(n - 1, inv_sum)
-                n_due = n // 2 if n < LAST_LOAD_STEP else n // 2 + 2 if n < B - LEAD + 1 else n
+                n_due = max(n - 6, 0) if n < B - LEAD + 1 else n
                 for b in range(n_stored, n_due):
                     rows = out[b].rearrange("(i a) h -> a i h", a=P)
                     for tiles in (slice(2, 4), slice(0, 2)) if b == B - 1 else (slice(0, 4),):

@@ -29,7 +29,7 @@ E_W = [2 * P * (i // 2 + 1) for i in range(NT)]
 E_OFF = [sum(E_W[:i]) for i in range(NT)]
 E_COLS = sum(E_W)
 
-SKEW_PAD = 8
+SKEW_PAD = 16
 SKEW_PITCH = ROW_COLS + SKEW_PAD
 SLOT = P * SKEW_PITCH
 N_SLOTS = 3
@@ -118,7 +118,9 @@ def tile_relativeattentionhead_pa_t_kernel(tc, x, q, k, Wv, rel_emb, out):
         q_raw, k_raw, x_raw = {}, {}, {}
         q_t, k_t, rel_skewed = {}, {}, {}
         rel_words = const.tile([P, L], F32)
-        rel_t = halves(rel_words)
+        rel_first = halves(rel_words)
+        rel_runs = const.tile([P, 2, L], BF16)
+        rel_t = rel_runs[:].rearrange("w h r -> w r h")
         x_grouped, x_codes, x_scales, v_grouped, v_codes, v_scales = {}, {}, {}, {}, {}, {}
         neg_max, row_sum, e_grouped, e_codes, e_scales, result = {}, {}, {}, {}, {}, {}
 
@@ -147,7 +149,7 @@ def tile_relativeattentionhead_pa_t_kernel(tc, x, q, k, Wv, rel_emb, out):
         def transpose_x(b, r):
             if r == 0:
                 x_grouped[b] = work.tile([P, L * X_PASSES * 4], BF16, align_bytes=64, name="x_grouped")
-            copy = nc.scalar.copy if r < (2 if b < B - 1 else 3) else nc.vector.tensor_copy
+            copy = nc.scalar.copy if r < (2 if b < B - 1 else 4) else nc.vector.tensor_copy
             features_to_partitions(x_raw[b], NT, x_grouped[b], r // 2, r % 2, copy)
 
         def q_times(acc, b, i, other, cols):
@@ -167,7 +169,7 @@ def tile_relativeattentionhead_pa_t_kernel(tc, x, q, k, Wv, rel_emb, out):
                 q_times(acc[:, col : col + ROW_W[i]], b, i, k_t[b], slice(0, ROW_W[i]))
             return acc
 
-        def q_times_rel(b, group):
+        def q_times_rel(b, group, rel_t):
             acc = psum.tile([P, L], F32, tag="bank")
             for i in group:
                 col = ROW_OFF[i] - ROW_OFF[group[0]]
@@ -259,7 +261,7 @@ def tile_relativeattentionhead_pa_t_kernel(tc, x, q, k, Wv, rel_emb, out):
                 if b_e >= 0 and r != 1:
                     transpose_e(b_e, 2 - r, nc.vector.tensor_copy if b_e == B - 1 and r == 0 else nc.scalar.copy)
                 if b_rel < B:
-                    park_relative_rows(b_rel, group, q_times_rel(b_rel, group), nc.scalar.copy)
+                    park_relative_rows(b_rel, group, q_times_rel(b_rel, group, rel_t), nc.scalar.copy)
                 if n < B:
                     negated_scores(n, group, acc_k)
                     if r >= 1:
@@ -341,24 +343,27 @@ def tile_relativeattentionhead_pa_t_kernel(tc, x, q, k, Wv, rel_emb, out):
             load_x(0)
             load_q(2)
             w_raw = load_blocks(raw_x, Wv, H // P, 1)
+            load_k(0)
+            load_k(1)
+            load_q(3)
 
             head_to_partitions(rel_raw, rel_words, nc.scalar.copy)
             transpose_q(0, nc.vector.tensor_copy)
 
-            def relative_term(b):
+            nc.vector.tensor_copy(out=rel_runs[:], in_=rel_first.rearrange("w r h -> w h r"))
+
+            def relative_term(b, rel_t):
                 for r, group in enumerate(GROUPS):
-                    park_relative_rows(b, group, q_times_rel(b, group), nc.vector.tensor_copy if r == 1 else nc.scalar.copy)
+                    copy = nc.vector.tensor_copy if r == 1 else nc.scalar.copy
+                    park_relative_rows(b, group, q_times_rel(b, group, rel_t), copy)
                 send_rows(b)
 
-            relative_term(0)
+            relative_term(0, rel_first)
             load_x(1)
-            load_q(3)
-            load_k(0)
-            load_k(1)
             transpose_q(1, nc.vector.tensor_copy)
             for r in range(NT):
                 transpose_x(0, r)
-            relative_term(1)
+            relative_term(1, rel_t)
             fetch_skewed(0)
             load_x(2)
             transpose_q(2, nc.vector.tensor_copy)
@@ -369,7 +374,7 @@ def tile_relativeattentionhead_pa_t_kernel(tc, x, q, k, Wv, rel_emb, out):
             w_codes = const.tile([P, X_PASSES * H], U32, align_bytes=64)
             w_scales = const.tile([P, X_PASSES * H], U8, align_bytes=64)
             nc.vector.quantize_mx(out=w_codes[:].bitcast(FP8X4), scales=w_scales[:], in_=w_grouped[:])
-            relative_term(2)
+            relative_term(2, rel_t)
             load_q(4)
             for r in range(NT):
                 transpose_x(1, r)

from contextlib import ExitStack

import concourse.mybir as mybir
from concourse.masks import make_identity

F32 = mybir.dt.float32
BF16 = mybir.dt.bfloat16
U32 = mybir.dt.uint32
U8 = mybir.dt.uint8
I32 = mybir.dt.int32
FP8X4 = mybir.dt.float8_e4m3fn_x4
ALU = mybir.AluOpType
ACT = mybir.ActivationFunctionType

B, L, E, H = 16, 512, 1024, 256
P = 128
NT = L // P
K_PASS = 4 * P
X_PASSES = E // K_PASS
FLOPS = 2 * B * L * (E * H + 3 * L * H)

GROUPS = ((3,), (2, 0), (1,))
ROW_W = [P * (i + 1) for i in range(NT)]
ROW_ORDER = [i for group in GROUPS for i in group]
ROW_OFF = [sum(ROW_W[j] for j in ROW_ORDER[: ROW_ORDER.index(i)]) for i in range(NT)]
ROW_COLS = sum(ROW_W)

E_W = [2 * P * (i // 2 + 1) for i in range(NT)]
E_OFF = [sum(E_W[:i]) for i in range(NT)]
E_COLS = sum(E_W)

SKEW_PAD = 16
SKEW_PITCH = ROW_COLS + SKEW_PAD
SLOT = P * SKEW_PITCH
N_SLOTS = 3
X_LEAD = 2
LEAD = 3
assert N_SLOTS * SLOT <= (LEAD + 1) * L * H

MASKED = -(2.0**100)


def slot_start(b):
    return B * L * H - ((B - 1 - b) % N_SLOTS + 1) * SLOT


def tile_relativeattentionhead_pa_t_kernel(tc, x, q, k, Wv, rel_emb, out):
    nc = tc.nc
    out_flat = out.rearrange("b l h -> (b l h)")

    with ExitStack() as ctx:
        const = ctx.enter_context(tc.tile_pool(name="const", bufs=1))
        raw_x = ctx.enter_context(tc.tile_pool(name="raw_x", bufs=4))
        raw_qk = ctx.enter_context(tc.tile_pool(name="raw_qk", bufs=8))
        heads = ctx.enter_context(tc.tile_pool(name="heads", bufs=LEAD + 2))
        skewed = ctx.enter_context(tc.tile_pool(name="skewed", bufs=LEAD + 1))
        results = ctx.enter_context(tc.tile_pool(name="results", bufs=11))
        work = ctx.enter_context(tc.tile_pool(name="work", bufs=2))
        keep_v = ctx.enter_context(tc.tile_pool(name="keep_v", bufs=4))
        small = ctx.enter_context(tc.tile_pool(name="small", bufs=3))
        psum = ctx.enter_context(tc.psum_pool(name="psum", bufs=7))
        psum_low = ctx.enter_context(tc.psum_pool(name="psum_low", bufs=1))

        zeros = const.tile([P, L], BF16)
        nc.vector.memset(zeros[:].bitcast(I32), 0)
        idle = psum.tile([P, L], F32, tag="bank")
        for i in range(4):
            nc.tensor.matmul(out=idle[:], lhsT=zeros[:, 0:P], rhs=zeros[:], start=True, stop=True)

        ident_f32 = const.tile([P, P], F32)
        make_identity(nc, ident_f32[:])

        rel_rows = [const.tile([P, SKEW_PITCH], F32, name="rel_rows%d" % j) for j in range(N_SLOTS)]
        for j in range(N_SLOTS):
            nc.vector.memset(rel_rows[j][:, ROW_COLS:SKEW_PITCH], 0.0)

        e_rows = [const.tile([P, E_COLS], BF16, name="e_rows%d" % j) for j in range(2)]
        for j in range(2):
            nc.vector.memset(e_rows[j][:].bitcast(I32), 0)
        turned_low = psum_low.tile([P, 2, 2, P], F32)
        for j in range(2):
            nc.tensor.transpose(turned_low[:, j, 1, :], zeros[:].bitcast(F32)[:, 0:P], ident_f32[:])

        def load_rows(pool, rows, per_partition):
            raw = pool.tile([P, per_partition * rows.shape[1]], BF16, tag="raw")
            nc.sync.dma_start(out=raw[:], in_=rows.rearrange("(p t) c -> p (t c)", t=per_partition))
            return raw

        def load_blocks(pool, rows, blocks, neighbours):
            n_cols = blocks * neighbours * rows.shape[1]
            raw = pool.tile([P, n_cols], BF16, tag="raw")
            nc.sync.dma_start(
                out=raw[:].rearrange("p (u w) -> p u w", u=blocks),
                in_=rows.rearrange("(u p h) c -> p u (h c)", u=blocks, h=neighbours),
            )
            return raw

        def head_to_partitions(raw, words, copy):
            raw_words = raw[:].bitcast(F32)
            turned = psum.tile([P, NT, P], F32, tag="bank")
            for t in range(NT):
                nc.tensor.transpose(turned[:, t, :], raw_words[:, t * P : (t + 1) * P], ident_f32[:])
            copy(out=words[:].rearrange("w (p t) -> w p t", t=NT), in_=turned[:].rearrange("w t p -> w p t"))

        def halves(words):
            return words[:].bitcast(BF16).rearrange("w (r h) -> w r h", h=2)

        def features_to_partitions(raw, slots, grouped, g, a, copy):
            raw_words = raw[:].bitcast(F32)
            dest = grouped[:].bitcast(F32).rearrange("w (g s p u) -> w g s p u", g=X_PASSES, s=slots, u=2)
            turned = psum.tile([P, 2, 2, P], F32, tag="bank")
            for j in range(2):
                for u in range(2):
                    col = ((2 * a + j) * X_PASSES * 2 + g * 2 + u) * P
                    nc.tensor.transpose(turned[:, j, u, :], raw_words[:, col : col + P], ident_f32[:])
            copy(out=dest[:, g, 2 * a : 2 * a + 2, :, :], in_=turned[:].rearrange("w s u p -> w s p u"))

        q_raw, k_raw, x_raw = {}, {}, {}
        q_t, k_t, rel_skewed = {}, {}, {}
        rel_words = const.tile([P, L], F32)
        rel_first = halves(rel_words)
        rel_runs = const.tile([P, 2, L], BF16)
        rel_t = rel_runs[:].rearrange("w h r -> w r h")
        x_grouped, x_codes, x_scales, v_grouped, v_codes, v_scales = {}, {}, {}, {}, {}, {}
        neg_max, row_sum, e_grouped, e_codes, e_scales, result = {}, {}, {}, {}, {}, {}

        def load_q(b):
            if b < B:
                q_raw[b] = load_rows(raw_qk, q[b], NT)

        def load_k(b):
            if b < B:
                k_raw[b] = load_rows(raw_qk, k[b], NT)

        def load_x(b):
            if b < B:
                x_raw[b] = load_blocks(raw_x, x[b], 2, 2)

        def transpose_q(b, copy):
            words = heads.tile([P, L], F32, tag="q_words")
            head_to_partitions(q_raw[b], words, copy)
            q_t[b] = halves(words)

        def transpose_k(b, copy):
            words = heads.tile([P, L], F32, tag="k_words")
            head_to_partitions(k_raw[b], words, copy)
            k_t[b] = halves(words)

        def transpose_x(b, r):
            if r == 0:
                x_grouped[b] = work.tile([P, L * X_PASSES * 4], BF16, align_bytes=64, name="x_grouped")
            copy = nc.scalar.copy if r < (2 if b < B - 1 else 4) else nc.vector.tensor_copy
            features_to_partitions(x_raw[b], NT, x_grouped[b], r // 2, r % 2, copy)

        def q_times(acc, b, i, other, cols):
            for h in range(2):
                nc.tensor.matmul(
                    out=acc, lhsT=q_t[b][:, i * P : (i + 1) * P, h], rhs=other[:, cols, h], start=(h == 0), stop=(h == 1)
                )

        def group_columns(group):
            start = ROW_OFF[group[0]]
            return slice(start, start + sum(ROW_W[i] for i in group))

        def q_times_k(b, group):
            acc = psum.tile([P, L], F32, tag="bank")
            for i in group:
                col = ROW_OFF[i] - ROW_OFF[group[0]]
                q_times(acc[:, col : col + ROW_W[i]], b, i, k_t[b], slice(0, ROW_W[i]))
            return acc

        def q_times_rel(b, group, rel_t):
            acc = psum.tile([P, L], F32, tag="bank")
            for i in group:
                col = ROW_OFF[i] - ROW_OFF[group[0]]
                q_times(acc[:, col : col + ROW_W[i]], b, i, rel_t, slice(L - ROW_W[i], L))
            return acc

        def negated_scores(b, group, acc):
            cols = group_columns(group)
            neg_s = rel_skewed[b][:, cols]
            nc.vector.scalar_tensor_tensor(
                out=neg_s, in0=acc[:, 0 : cols.stop - cols.start], scalar=-1.0 / 16.0, in1=neg_s, op0=ALU.mult,
                op1=ALU.subtract,
            )

        def negated_maximum(b, i):
            neg_s = rel_skewed[b][:, ROW_OFF[i] : ROW_OFF[i] + ROW_W[i]]
            nc.vector.tensor_reduce(out=neg_max[b][:, i : i + 1], in_=neg_s, axis=mybir.AxisListType.X, op=ALU.min)

        def softmax_numerators(b, i):
            cols = slice(ROW_OFF[i], ROW_OFF[i] + ROW_W[i])
            nc.scalar.activation(
                out=e_rows[b % 2][:, E_OFF[i] : E_OFF[i] + ROW_W[i]], in_=rel_skewed[b][:, cols], func=ACT.Exp, bias=neg_max[b][:, i : i + 1],
                scale=-1.0, accum_out=row_sum[b][:, i : i + 1],
            )

        def park_relative_rows(b, group, acc, copy):
            rows = rel_rows[(B - 1 - b) % N_SLOTS]
            cols = group_columns(group)
            copy(out=rows[:, cols], in_=acc[:, 0 : cols.stop - cols.start])

        def send_rows(b):
            start = slot_start(b)
            nc.sync.dma_start(
                out=out_flat[start : start + SLOT].rearrange("(a u) -> a u", u=SKEW_PITCH),
                in_=rel_rows[(B - 1 - b) % N_SLOTS][:],
            )

        def fetch_skewed(b):
            start = slot_start(b) + P - 1
            shifted = out_flat[start : start + P * (SKEW_PITCH - 1)].rearrange("(a u) -> a u", u=SKEW_PITCH - 1)
            rel_skewed[b] = skewed.tile([P, ROW_COLS], F32, name="rel_skewed")
            nc.sync.dma_start(out=rel_skewed[b][:], in_=shifted[:, 0:ROW_COLS])
            diagonals = [(ROW_OFF[group[0]] + group[0] * P, len(group)) for group in GROUPS]
            for start, n_tiles in diagonals if b == 0 else reversed(diagonals):
                diagonal = rel_skewed[b][:, start : start + n_tiles * P]
                nc.gpsimd.affine_select(
                    out=diagonal, in_=diagonal, pattern=[[0, n_tiles], [-1, P]], compare_op=ALU.is_ge, fill=MASKED,
                    base=0, channel_multiplier=1,
                )

        def transpose_e(b, first, copy):
            words = e_rows[b % 2][:].bitcast(F32)
            turned = turned_low if first == 0 else psum.tile([P, 2, 2, P], F32, tag="bank")
            for j in range(2):
                for u in range(E_W[first + j] // (2 * P)):
                    col = (E_OFF[first + j] + 2 * P * u) // 2
                    nc.tensor.transpose(turned[:, j, u, :], words[:, col : col + P], ident_f32[:])
            dest = e_grouped[b][:].bitcast(F32).rearrange("p (i a u) -> p i a u", i=NT, u=2)
            copy(out=dest[:, first : first + 2, :, :], in_=turned[:].rearrange("p i u a -> p i a u"))

        def quantise(pool, grouped, name):
            n_words = grouped.shape[1] // 4
            codes = pool.tile([P, n_words], U32, align_bytes=64, name=name + "_codes")
            scales = pool.tile([P, n_words], U8, align_bytes=64, name=name + "_scales")
            nc.vector.quantize_mx(out=codes[:].bitcast(FP8X4), scales=scales[:], in_=grouped)
            return codes, scales

        def quantise_e(b, tiles):
            if b not in e_codes:
                e_codes[b] = work.tile([P, L], U32, align_bytes=64, name="e_codes")
                e_scales[b] = work.tile([P, L], U8, align_bytes=64, name="e_scales")
            cols = slice(tiles.start * P, tiles.stop * P)
            nc.vector.quantize_mx(
                out=e_codes[b][:, cols].bitcast(FP8X4), scales=e_scales[b][:, cols],
                in_=e_grouped[b][:, tiles.start * P * NT : tiles.stop * P * NT],
            )

        def matmuls_and_transposes(n):
            b_e, b_rel, b_x, b_q, b_k = n - 1, n + LEAD, n + X_LEAD, n + LEAD + 1, n + 1
            b_v = n + X_LEAD - 2
            if n < B:
                neg_max[n] = small.tile([P, NT], F32, name="neg_max")
                row_sum[n] = small.tile([P, NT], F32, name="row_sum")
            if b_e >= 0:
                e_grouped[b_e] = work.tile([P, L * NT], BF16, align_bytes=64, name="e_grouped")
            for r, group in enumerate(GROUPS):
                if n < B:
                    acc_k = q_times_k(n, group)
                if b_e >= 0 and r != 1:
                    transpose_e(b_e, 2 - r, nc.vector.tensor_copy if b_e == B - 1 and r == 0 else nc.scalar.copy)
                if b_rel < B:
                    park_relative_rows(b_rel, group, q_times_rel(b_rel, group, rel_t), nc.scalar.copy)
                if n < B:
                    negated_scores(n, group, acc_k)
                    if r >= 1:
                        for i in GROUPS[r - 1]:
                            negated_maximum(n, i)
                    if r >= 2:
                        for i in GROUPS[r - 2]:
                            softmax_numerators(n, i)
                for j in ((), (0, 1), (2, 3))[r] if b_x < B else ():
                    transpose_x(b_x, j)
                if b_k < B and r == 0:
                    transpose_k(b_k, nc.scalar.copy)
                if b_q < B and r == 2:
                    transpose_q(b_q, nc.scalar.copy)
                if b_v < B and r == 1:
                    v_codes[b_v], v_scales[b_v] = quantise(keep_v, v_grouped[b_v][:].rearrange("p c t -> p (c t)"), "v")
                if b_e == B - 1 and r != 1:
                    quantise_e(b_e, slice(2 - r, 4 - r))
                elif b_e >= 0 and r == 2:
                    quantise_e(b_e, slice(0, NT))
            if n < B:
                for i in GROUPS[2]:
                    negated_maximum(n, i)
                for group in GROUPS[1:]:
                    for i in group:
                        softmax_numerators(n, i)

        def project_v(b):
            v_grouped[b] = work.tile([P, H, NT], BF16, align_bytes=64, name="v_grouped")
            for half in range(H // P):
                acc = psum.tile([P, NT, P], F32, tag="bank")
                for t in range(NT):
                    for g in range(X_PASSES):
                        tok = slice(g * L + t * P, g * L + (t + 1) * P)
                        col = slice(g * H + half * P, g * H + (half + 1) * P)
                        nc.tensor.matmul_mx(
                            out=acc[:, t, :],
                            lhsT=x_codes[b][:, tok].bitcast(FP8X4),
                            lhsT_scale=x_scales[b][:, tok],
                            rhs=w_codes[:, col].bitcast(FP8X4),
                            rhs_scale=w_scales[:, col],
                            start=(g == 0),
                            stop=(g == X_PASSES - 1),
                        )
                nc.scalar.copy(out=v_grouped[b][:, half * P : (half + 1) * P, :], in_=acc[:].rearrange("p t c -> p c t"))

        def weighted_sum(b, inv_sum):
            result[b] = results.tile([P, NT, H], F32, name="result")
            for pair in reversed(range(NT // 2)):
                tiles = slice(2 * pair, 2 * pair + 2)
                acc = psum.tile([P, 2, H], F32, tag="bank")
                for j in range(2):
                    i = 2 * pair + j
                    nc.tensor.matmul_mx(
                        out=acc[:, j, :],
                        lhsT=e_codes[b][:, i * P : (i + 1) * P].bitcast(FP8X4),
                        lhsT_scale=e_scales[b][:, i * P : (i + 1) * P],
                        rhs=v_codes[b][:].bitcast(FP8X4),
                        rhs_scale=v_scales[b][:],
                        start=True,
                        stop=True,
                    )
                if pair == 0 and b + 1 + LEAD >= B:
                    for j in range(2):
                        i = 2 * pair + j
                        nc.scalar.activation(
                            out=result[b][:, i, :], in_=acc[:, j, :], func=ACT.Copy, scale=inv_sum[:, i : i + 1]
                        )
                else:
                    nc.vector.tensor_tensor(
                        out=result[b][:, tiles, :], in0=acc[:], in1=inv_sum[:, tiles].unsqueeze(2).to_broadcast([P, 2, H]),
                        op=ALU.mult,
                    )

        with tc.manual_schedule():
            rel_raw = load_rows(raw_qk, rel_emb, NT)
            load_q(0)
            load_q(1)
            load_x(0)
            load_q(2)
            w_raw = load_blocks(raw_x, Wv, H // P, 1)
            load_k(0)
            load_k(1)
            load_q(3)

            head_to_partitions(rel_raw, rel_words, nc.scalar.copy)
            transpose_q(0, nc.vector.tensor_copy)

            nc.vector.tensor_copy(out=rel_runs[:], in_=rel_first.rearrange("w r h -> w h r"))

            def relative_term(b, rel_t):
                for r, group in enumerate(GROUPS):
                    copy = nc.vector.tensor_copy if r == 1 else nc.scalar.copy
                    park_relative_rows(b, group, q_times_rel(b, group, rel_t), copy)
                send_rows(b)

            relative_term(0, rel_first)
            load_x(1)
            transpose_q(1, nc.vector.tensor_copy)
            for r in range(NT):
                transpose_x(0, r)
            relative_term(1, rel_t)
            fetch_skewed(0)
            load_x(2)
            transpose_q(2, nc.vector.tensor_copy)
            x_codes[0], x_scales[0] = quantise(work, x_grouped[0][:], "x")
            w_grouped = const.tile([P, X_PASSES * H * 4], BF16, align_bytes=64)
            for g in range(X_PASSES):
                features_to_partitions(w_raw, H // P, w_grouped, g, 0, nc.vector.tensor_copy)
            w_codes = const.tile([P, X_PASSES * H], U32, align_bytes=64)
            w_scales = const.tile([P, X_PASSES * H], U8, align_bytes=64)
            nc.vector.quantize_mx(out=w_codes[:].bitcast(FP8X4), scales=w_scales[:], in_=w_grouped[:])
            relative_term(2, rel_t)
            load_q(4)
            for r in range(NT):
                transpose_x(1, r)
            transpose_k(0, nc.scalar.copy)
            transpose_q(3, nc.scalar.copy)
            x_codes[1], x_scales[1] = quantise(work, x_grouped[1][:], "x")
            project_v(0)
            fetch_skewed(1)
            load_k(2)
            load_x(3)
            load_q(5)

            n_stored = 0
            for n in range(B + 1):
                if n + LEAD - 1 < B:
                    fetch_skewed(n + LEAD - 1)
                matmuls_and_transposes(n)
                if n + LEAD < B:
                    send_rows(n + LEAD)
                load_q(n + LEAD + 3)
                load_k(n + 3)
                load_x(n + X_LEAD + 2)

                if n >= 1:
                    inv_sum = small.tile([P, NT], F32)
                    nc.vector.reciprocal(out=inv_sum[:], in_=row_sum[n - 1][:])
                if n + X_LEAD < B:
                    x_codes[n + X_LEAD], x_scales[n + X_LEAD] = quantise(work, x_grouped[n + X_LEAD][:], "x")
                if n + X_LEAD - 1 < B:
                    project_v(n + X_LEAD - 1)
                if n >= 1:
                    weighted_sum(n - 1, inv_sum)
                n_due = max(n - 6, 0) if n < B - LEAD + 1 else n
                for b in range(n_stored, n_due):
                    rows = out[b].rearrange("(i a) h -> a i h", a=P)
                    for tiles in (slice(2, 4), slice(0, 2)) if b == B - 1 else (slice(0, 4),):
                        nc.sync.dma_start(out=rows[:, tiles, :], in_=result[b][:, tiles, :])
                n_stored = n_due
